import numpy as np
import ml_dtypes


def mxq(x, axis, fmt="e4m3"):
    dtype, down = {"e4m3": (ml_dtypes.float8_e4m3fn, 7), "e5m2": (ml_dtypes.float8_e5m2, 14)}[fmt]
    v = np.moveaxis(np.asarray(x, np.float32).astype(ml_dtypes.bfloat16).astype(np.float64), axis, -1)
    blocks = v.reshape(v.shape[:-1] + (-1, 32))
    amax = np.abs(blocks).max(-1, keepdims=True)
    byte = np.maximum(np.where(amax > 0, np.frexp(amax)[1] - 1 + 127, 0) - down, 1)
    scale = np.exp2(byte - 127.0)
    codes = (blocks / scale).astype(np.float32).astype(dtype).astype(np.float64)
    return np.moveaxis((codes * scale).reshape(v.shape), -1, axis)


WIDE = False


def mx_kscale(k):
    if not WIDE:
        return np.ones(k)
    levels = np.array([10, -10, 5, -5, 0])
    if k % 512:
        return np.exp2(np.random.permutation(np.resize(levels, k // 32))).repeat(32)
    a = np.empty((k // 512, 16))
    for p in range(k // 512):
        a[p, :8] = np.random.permutation(np.resize(levels, 8))
        for g in range(8):
            far = levels[np.abs(levels - a[p, g]) >= 10]
            a[p, g + 8] = far[np.random.randint(len(far))]
    return np.exp2(a.ravel()).repeat(32)


BF16 = ml_dtypes.bfloat16


def bf(x):
    return np.asarray(x, np.float32).astype(BF16)


def f64(x):
    return np.asarray(x).astype(np.float64)


B, S, D, E, F = 4, 1024, 1024, 256, 4096
EPS = 1e-5


def layernorm(x, g, b):
    m = x.mean(-1, keepdims=True)
    v = ((x - m) ** 2).mean(-1, keepdims=True)
    return (x - m) * (1.0 / np.sqrt(v + EPS)) * g + b


def rotate_half(x):
    return np.concatenate([-x[..., ::2], x[..., 1::2]], axis=-1)


def sinu_pos_emb(dim, length):
    inv_freq = 1.0 / 10000.0 ** (np.arange(0, dim, 2) / dim)
    sp = np.arange(length)[:, None] * inv_freq[None, :]
    return np.concatenate([np.sin(sp), np.cos(sp)], axis=-1)


def setup_inputs():
    s = mx_kscale(D)
    return {"src": bf(np.random.standard_normal((B, S, D)) + 0.5),
            "Wqkv": bf(np.random.standard_normal((3 * E, D)) / np.sqrt(D) / s[None, :]),
            "bqkv": bf(0.1 * np.random.standard_normal(3 * E)),
            "g1": bf((1.0 + 0.1 * np.random.standard_normal(D)) * s),
            "be1": bf(0.1 * np.random.standard_normal(D) * s)}


def reference(src, Wqkv, bqkv, g1, be1):
    xn = layernorm(f64(src), f64(g1), f64(be1))
    qkv = (mxq(xn, 2, "e4m3") @ mxq(f64(Wqkv), 1, "e4m3").T) + f64(bqkv)
    Q, K, V = qkv[..., :E], qkv[..., E:2 * E], qkv[..., 2 * E:]
    emb = sinu_pos_emb(E, S)
    c, s = np.cos(emb), np.sin(emb)
    Q = Q * c + rotate_half(Q) * s
    K = K * c - rotate_half(K) * s
    return Q, K, V

@@ -1,0 +1,327 @@
+import math
+
+import concourse.mybir as mybir
+from concourse.masks import make_identity
+
+F32 = mybir.dt.float32
+BF16 = mybir.dt.bfloat16
+I32 = mybir.dt.int32
+U32 = mybir.dt.uint32
+U8 = mybir.dt.uint8
+FP8X4 = mybir.dt.float8_e4m3fn_x4
+ALU = mybir.AluOpType
+ACT = mybir.ActivationFunctionType
+
+P = 128
+BATCH = 4
+SEQ = 1024
+D = 1024
+E = 256
+HALF = E // 2
+N_OUT = 3 * E
+EPS = 1e-5
+
+PACK = 4
+K_PASS = P * PACK
+PASSES = D // K_PASS
+CHUNKS = D // P
+ROUNDS = SEQ // P
+TOKENS = BATCH * P
+BN_CHUNK = 512
+T_BANKS = 4
+
+FREQ_RATIO = 10000.0 ** (-1.0 / HALF)
+ROUND_MAGIC = 12582912.0
+
+FLOPS = 2 * BATCH * SEQ * D * N_OUT
+
+
+def build_position_tables(nc, work, tables):
+    quarter_turn = work.tile([P, 1], F32)
+    nc.vector.memset(quarter_turn[:], 1.0)
+    nc.vector.tensor_scalar(out=quarter_turn[:], in0=quarter_turn[:], scalar1=0.5 * math.pi, scalar2=None, op0=ALU.mult)
+    position = work.tile([P, ROUNDS, 1], I32)
+    nc.gpsimd.iota(position[:], pattern=[[P, ROUNDS]], base=0, channel_multiplier=1)
+    turns = work.tile([P, ROUNDS, HALF], F32)
+    nc.vector.tensor_scalar(out=turns[:, :, 0:1], in0=position[:], scalar1=0.5 / math.pi, scalar2=None, op0=ALU.mult)
+    for doubling in range(7):
+        n = 2**doubling
+        nc.vector.tensor_scalar(
+            out=turns[:, :, n : 2 * n], in0=turns[:, :, 0:n], scalar1=FREQ_RATIO**n, scalar2=None, op0=ALU.mult
+        )
+    whole = work.tile([P, ROUNDS, HALF], F32)
+    nc.vector.tensor_scalar(out=whole[:], in0=turns[:], scalar1=ROUND_MAGIC, scalar2=None, op0=ALU.add)
+    minus_f = work.tile([P, ROUNDS, HALF], F32)
+    nc.vector.scalar_tensor_tensor(
+        out=minus_f[:], in0=whole[:], scalar=ROUND_MAGIC, in1=turns[:], op0=ALU.subtract, op1=ALU.subtract
+    )
+    emb = work.tile([P, ROUNDS, E], F32)
+    nc.scalar.activation(out=emb[:, :, 0:HALF], in_=minus_f[:], func=ACT.Sin, scale=-2.0 * math.pi)
+    nc.scalar.activation(out=minus_f[:], in_=minus_f[:], func=ACT.Abs)
+    nc.scalar.activation(
+        out=emb[:, :, HALF:E], in_=minus_f[:], func=ACT.Sin, scale=-2.0 * math.pi, bias=quarter_turn[:]
+    )
+    nc.scalar.activation(out=tables[:, :, 0, :], in_=emb[:], func=ACT.Sin, bias=quarter_turn[:])
+    nc.scalar.activation(out=tables[:, :, 1, 0:HALF], in_=emb[:, :, 0:HALF], func=ACT.Sin, scale=-1.0)
+    nc.scalar.activation(out=tables[:, :, 1, HALF:E], in_=emb[:, :, HALF:E], func=ACT.Sin)
+
+
+def tile_rotaryembeddingtransformerlayer_pa_t_kernel(
+    tc, src, Wqkv, bqkv, g1, be1, out_0, out_1, out_2
+):
+    nc = tc.nc
+    with (
+        tc.tile_pool(name="const", bufs=1) as const,
+        tc.tile_pool(name="work", bufs=1) as work,
+        tc.tile_pool(name="xin", bufs=3) as xin,
+        tc.tile_pool(name="small", bufs=3) as small,
+        tc.tile_pool(name="norm", bufs=2) as norm,
+        tc.tile_pool(name="planes", bufs=1) as plane_pool,
+        tc.tile_pool(name="quant", bufs=2) as quant,
+        tc.tile_pool(name="mix", bufs=2) as mix,
+        tc.psum_pool(name="psum_t", bufs=T_BANKS) as psum_t,
+        tc.psum_pool(name="psum_acc", bufs=3) as psum_acc,
+        tc.psum_pool(name="psum_tab", bufs=1) as psum_tab,
+        tc.manual_schedule(),
+    ):
+        ident_f32 = const.tile([P, P], F32)
+        minus_half = const.tile([P, BATCH], F32)
+        gain = const.tile([P, 2 * CHUNKS], F32)
+        bias_all = const.tile([P, N_OUT], BF16)
+        w_codes = const.tile([P, PASSES, N_OUT], U32, align_bytes=64)
+        w_scales = const.tile([P, PASSES, N_OUT], U8, align_bytes=64)
+        tables = const.tile([P, ROUNDS, 2, E], F32)
+        w_rows = work.tile([P, N_OUT // P, D], BF16)
+        g1_bf16 = work.tile([P, PASSES, PACK], BF16)
+        be1_bf16 = work.tile([P, PASSES, PACK], BF16)
+
+        x_of, moments_of, rstd_of, shift_of, z_of, zT_of = {}, {}, {}, {}, {}, {}
+        planes_of, grouped_of, codes_of, scales_of = {}, {}, {}, {}
+        qk_of, straight_of, turned_of = {}, {}, {}
+
+        def live(t):
+            return 0 <= t < ROUNDS
+
+        def rows(t):
+            return slice(t * P, (t + 1) * P)
+
+        def load(t):
+            x_of[t] = xin.tile([P, BATCH, D], BF16, name="x")
+            nc.sync.dma_start(out=x_of[t][:], in_=src[:, rows(t), :].rearrange("b p k -> p b k"))
+
+        def statistics(t):
+            x = x_of[t]
+            stats = small.tile([P, BATCH, D // BN_CHUNK, 6], F32, name="stats")
+            mean_var = small.tile([P, BATCH, 2], F32, name="mean_var")
+            for b in range(BATCH):
+                for h in range(D // BN_CHUNK):
+                    nc.vector.bn_stats(out=stats[:, b, h, :], in_=x[:, b, h * BN_CHUNK : (h + 1) * BN_CHUNK])
+            for b in range(BATCH):
+                nc.vector.bn_aggr(out=mean_var[:, b, :], in_=stats[:, b, :, :].rearrange("p h s -> p (h s)"))
+            moments_of[t] = mean_var
+
+        def scale_and_shift(t):
+            var_eps = small.tile([P, BATCH], F32, name="var_eps")
+            nc.gpsimd.tensor_scalar(
+                out=var_eps[:], in0=moments_of[t][:, :, 1], scalar1=1.0, scalar2=EPS, op0=ALU.mult, op1=ALU.add
+            )
+            minus_mean = small.tile([P, BATCH], F32, name="minus_mean")
+            nc.gpsimd.tensor_scalar(
+                out=minus_mean[:], in0=moments_of[t][:, :, 0], scalar1=-1.0, scalar2=0.0, op0=ALU.mult, op1=ALU.add
+            )
+            rstd_of[t] = small.tile([P, BATCH], F32, name="rstd")
+            nc.gpsimd.tensor_tensor(out=rstd_of[t][:], in0=var_eps[:], in1=minus_half[:], op=ALU.pow)
+            shift_of[t] = small.tile([P, BATCH], F32, name="shift")
+            nc.gpsimd.tensor_tensor(out=shift_of[t][:], in0=minus_mean[:], in1=rstd_of[t][:], op=ALU.mult)
+
+        def by_chunk(z):
+            return z.rearrange("p (c j m) -> p c j m", c=PASSES, j=PACK)
+
+        def by_slot(x):
+            return x.rearrange("p (c m j) -> p c j m", c=PASSES, j=PACK)
+
+        def normalise_last(t):
+            z_of[t] = norm.tile([P, BATCH, D], F32, name="z")
+            b = BATCH - 1
+            nc.gpsimd.tensor_scalar(
+                out=by_chunk(z_of[t][:, b, :]), in0=by_slot(x_of[t][:, b, :]), scalar1=rstd_of[t][:, b : b + 1],
+                scalar2=shift_of[t][:, b : b + 1], op0=ALU.mult, op1=ALU.add,
+            )
+
+        def normalise(t):
+            for b in range(BATCH - 1):
+                nc.scalar.activation(
+                    out=by_chunk(z_of[t][:, b, :]), in_=by_slot(x_of[t][:, b, :]), func=ACT.Identity,
+                    scale=rstd_of[t][:, b : b + 1], bias=shift_of[t][:, b : b + 1],
+                )
+
+        def transpose(t, kc):
+            zT_of[t, kc] = psum_t.tile([P, TOKENS], F32, name="zT")
+            for b in range(BATCH):
+                nc.tensor.transpose(
+                    zT_of[t, kc][:, b * P : (b + 1) * P], z_of[t][:, b, kc * P : (kc + 1) * P], ident_f32[:]
+                )
+
+        def gain_out(t, kc):
+            if kc == 0:
+                planes_of[t] = plane_pool.tile([P, CHUNKS, TOKENS], BF16, name="planes")
+            nc.scalar.activation(
+                out=planes_of[t][:, kc, :], in_=zT_of[t, kc][:], func=ACT.Identity,
+                scale=gain[:, kc : kc + 1], bias=gain[:, CHUNKS + kc : CHUNKS + kc + 1],
+            )
+
+        def regroup(t, c):
+            if c == 0:
+                grouped_of[t] = quant.tile([P, PASSES, TOKENS, PACK], BF16, name="grouped", align_bytes=64)
+            nc.scalar.copy(
+                out=grouped_of[t][:, c, :, :].rearrange("p (m i) j -> p m j i", i=4),
+                in_=planes_of[t][:, PACK * c : PACK * (c + 1), :].rearrange("p j (m i) -> p m j i", i=4),
+            )
+
+        def quantise(t):
+            codes_of[t] = quant.tile([P, PASSES, TOKENS], U32, name="codes", align_bytes=64)
+            scales_of[t] = quant.tile([P, PASSES, TOKENS], U8, name="scales", align_bytes=64)
+            nc.vector.quantize_mx(
+                out=codes_of[t][:].rearrange("p c w -> p (c w)").bitcast(FP8X4),
+                scales=scales_of[t][:].rearrange("p c w -> p (c w)"),
+                in_=grouped_of[t][:].rearrange("p c w j -> p (c w j)"),
+            )
+
+        def multiply(acc, t, b, lo, hi):
+            tok = slice(b * P, (b + 1) * P)
+            for c in range(PASSES):
+                nc.tensor.matmul_mx(
+                    out=acc,
+                    lhsT=codes_of[t][:, c, tok].bitcast(FP8X4), lhsT_scale=scales_of[t][:, c, tok],
+                    rhs=w_codes[:, c, lo:hi].bitcast(FP8X4), rhs_scale=w_scales[:, c, lo:hi],
+                    start=(c == 0), stop=(c == PASSES - 1),
+                )
+
+        def turn(engine, t, pair, sines):
+            engine.tensor_tensor(
+                out=turned_of[t][:, pair].rearrange("p b q (h i) -> p (b q) h i", h=2),
+                in0=qk_of[t][:, pair].rearrange("p b q (i h) -> p (b q) h i", h=2),
+                in1=sines.rearrange("p (h i) -> p h i", h=2).unsqueeze(1).to_broadcast([P, 4, 2, HALF]),
+                op=ALU.mult,
+            )
+
+        def project(t):
+            tab_ps = psum_tab.tile([P, 2, E], F32, name="tab_ps")
+            nc.tensor.matmul(
+                out=tab_ps[:].rearrange("p s e -> p (s e)"), lhsT=ident_f32[:],
+                rhs=tables[:, t, :, :].rearrange("p s e -> p (s e)"), start=True, stop=True,
+            )
+            qk_of[t] = mix.tile([P, BATCH, 2, E], F32, name="qk")
+            straight_of[t] = mix.tile([P, BATCH, 2, E], F32, name="straight")
+            turned_of[t] = mix.tile([P, BATCH, 2, E], F32, name="turned")
+            v = mix.tile([P, BATCH, E], F32, name="v")
+            for b in range(BATCH):
+                acc_qk = psum_acc.tile([P, 2 * E], F32, name="acc_qk", tag="acc")
+                multiply(acc_qk[:], t, b, 0, 2 * E)
+                nc.vector.tensor_tensor(
+                    out=qk_of[t][:, b, :, :].rearrange("p q e -> p (q e)"), in0=acc_qk[:],
+                    in1=bias_all[:, 0 : 2 * E], op=ALU.add,
+                )
+                if b % 2 == 0:
+                    acc_v = psum_acc.tile([P, 2, E], F32, name="acc_v", tag="acc")
+                multiply(acc_v[:, b % 2, :], t, b, 2 * E, N_OUT)
+                if b % 2 == 1:
+                    pair = slice(b - 1, b + 1)
+                    nc.vector.tensor_tensor(
+                        out=v[:, pair, :], in0=acc_v[:],
+                        in1=bias_all[:, 2 * E : N_OUT].unsqueeze(1).to_broadcast([P, 2, E]), op=ALU.add,
+                    )
+                    nc.vector.tensor_tensor(
+                        out=straight_of[t][:, pair].rearrange("p b q e -> p (b q) e"),
+                        in0=qk_of[t][:, pair].rearrange("p b q e -> p (b q) e"),
+                        in1=tab_ps[:, 0, :].unsqueeze(1).to_broadcast([P, 4, E]),
+                        op=ALU.mult,
+                    )
+            turn(nc.vector, t, slice(2, 4), tab_ps[:, 1, :])
+            nc.sync.dma_start(out=out_2[:, rows(t), :].rearrange("b p e -> p b e"), in_=v[:])
+
+        def finish_mix(t):
+            straight, turned = straight_of[t], turned_of[t]
+            turn(nc.gpsimd, t, slice(0, 2), tables[:, t, 1, :])
+            for b in range(0, BATCH, 2):
+                pair = slice(b, b + 2)
+                for q, out, op in ((0, out_0, ALU.add), (1, out_1, ALU.subtract)):
+                    nc.gpsimd.tensor_tensor(
+                        out=straight[:, pair, q, :], in0=straight[:, pair, q, :], in1=turned[:, pair, q, :], op=op
+                    )
+                    nc.sync.dma_start(
+                        out=out[pair, rows(t), :].rearrange("b p e -> p b e"), in_=straight[:, pair, q, :]
+                    )
+
+        def prepare_gain():
+            nc.vector.tensor_copy(out=gain[:, 0:CHUNKS], in_=g1_bf16[:].rearrange("p c j -> p (c j)"))
+            nc.vector.tensor_copy(out=gain[:, CHUNKS : 2 * CHUNKS], in_=be1_bf16[:].rearrange("p c j -> p (c j)"))
+
+        def prepare_weights():
+            w_words = w_rows[:].rearrange("p r k -> p (r k)").bitcast(F32).rearrange("p (r w) -> p r w", r=N_OUT // P)
+            w_grouped = work.tile([P, PASSES, N_OUT, PACK], BF16, name="w_grouped", align_bytes=64)
+            for c in range(PASSES):
+                for pair in range(N_OUT // (2 * P)):
+                    wT = psum_acc.tile([P, 2, 2 * P], F32, name="wT", tag="acc")
+                    for u in range(2):
+                        for h in range(2):
+                            nc.tensor.transpose(
+                                wT[:, u, h * P : (h + 1) * P],
+                                w_words[:, 2 * pair + h, 2 * P * c + u : 2 * P * (c + 1) : 2],
+                                ident_f32[:],
+                            )
+                    nc.vector.tensor_copy(
+                        out=w_grouped[:, c, 2 * P * pair : 2 * P * (pair + 1), :]
+                        .rearrange("p n j -> p (n j)").bitcast(F32).rearrange("p (n u) -> p n u", u=2),
+                        in_=wT[:].rearrange("p u n -> p n u"),
+                    )
+            for c in range(PASSES):
+                for lo, hi in ((0, 2 * E), (2 * E, N_OUT)):
+                    nc.vector.quantize_mx(
+                        out=w_codes[:, c, lo:hi].bitcast(FP8X4),
+                        scales=w_scales[:, c, lo:hi],
+                        in_=w_grouped[:, c, lo:hi, :].rearrange("p n j -> p (n j)"),
+                    )
+
+        load(0)
+        nc.sync.dma_start(out=g1_bf16[:], in_=g1.rearrange("(c p j) -> p c j", c=PASSES, j=PACK))
+        nc.sync.dma_start(out=be1_bf16[:], in_=be1.rearrange("(c p j) -> p c j", c=PASSES, j=PACK))
+        load(1)
+        nc.sync.dma_start(out=w_rows[:], in_=Wqkv.rearrange("(r p) k -> p r k", p=P))
+        nc.sync.dma_start(out=bias_all[:], in_=bqkv.partition_broadcast(P))
+        load(2)
+        make_identity(nc, ident_f32[:])
+        nc.vector.memset(minus_half[:], -0.5)
+        build_position_tables(nc, work, tables)
+        prepare_gain()
+
+        for i in range(-2, ROUNDS + 1):
+            if live(i + 3) and i >= 0:
+                load(i + 3)
+            if live(i - 1):
+                quantise(i - 1)
+            if live(i):
+                for kc in range(CHUNKS - T_BANKS):
+                    gain_out(i, kc)
+                    transpose(i, kc + T_BANKS)
+            if live(i + 2):
+                statistics(i + 2)
+            if i == 0:
+                prepare_weights()
+            if live(i - 1):
+                project(i - 1)
+            if live(i):
+                for kc in range(CHUNKS - T_BANKS, CHUNKS):
+                    gain_out(i, kc)
+            if live(i + 1):
+                normalise(i + 1)
+                for kc in range(T_BANKS):
+                    transpose(i + 1, kc)
+            if live(i + 2):
+                scale_and_shift(i + 2)
+                normalise_last(i + 2)
+            if live(i - 1):
+                finish_mix(i - 1)
+            if live(i):
+                regroup(i, 0)
+                regroup(i, 1)

@@ -11,6 +11,7 @@ U8 = mybir.dt.uint8
 FP8X4 = mybir.dt.float8_e4m3fn_x4
 ALU = mybir.AluOpType
 ACT = mybir.ActivationFunctionType
+AX = mybir.AxisListType
 
 P = 128
 BATCH = 4
@@ -28,42 +29,14 @@ CHUNKS = D // P
 ROUNDS = SEQ // P
 TOKENS = BATCH * P
 BN_CHUNK = 512
-T_BANKS = 4
+BANK = 512
+T_BANKS = 3
+G_NORM = 4
 
 FREQ_RATIO = 10000.0 ** (-1.0 / HALF)
 ROUND_MAGIC = 12582912.0
 
 FLOPS = 2 * BATCH * SEQ * D * N_OUT
-
-
-def build_position_tables(nc, work, tables):
-    quarter_turn = work.tile([P, 1], F32)
-    nc.vector.memset(quarter_turn[:], 1.0)
-    nc.vector.tensor_scalar(out=quarter_turn[:], in0=quarter_turn[:], scalar1=0.5 * math.pi, scalar2=None, op0=ALU.mult)
-    position = work.tile([P, ROUNDS, 1], I32)
-    nc.gpsimd.iota(position[:], pattern=[[P, ROUNDS]], base=0, channel_multiplier=1)
-    turns = work.tile([P, ROUNDS, HALF], F32)
-    nc.vector.tensor_scalar(out=turns[:, :, 0:1], in0=position[:], scalar1=0.5 / math.pi, scalar2=None, op0=ALU.mult)
-    for doubling in range(7):
-        n = 2**doubling
-        nc.vector.tensor_scalar(
-            out=turns[:, :, n : 2 * n], in0=turns[:, :, 0:n], scalar1=FREQ_RATIO**n, scalar2=None, op0=ALU.mult
-        )
-    whole = work.tile([P, ROUNDS, HALF], F32)
-    nc.vector.tensor_scalar(out=whole[:], in0=turns[:], scalar1=ROUND_MAGIC, scalar2=None, op0=ALU.add)
-    minus_f = work.tile([P, ROUNDS, HALF], F32)
-    nc.vector.scalar_tensor_tensor(
-        out=minus_f[:], in0=whole[:], scalar=ROUND_MAGIC, in1=turns[:], op0=ALU.subtract, op1=ALU.subtract
-    )
-    emb = work.tile([P, ROUNDS, E], F32)
-    nc.scalar.activation(out=emb[:, :, 0:HALF], in_=minus_f[:], func=ACT.Sin, scale=-2.0 * math.pi)
-    nc.scalar.activation(out=minus_f[:], in_=minus_f[:], func=ACT.Abs)
-    nc.scalar.activation(
-        out=emb[:, :, HALF:E], in_=minus_f[:], func=ACT.Sin, scale=-2.0 * math.pi, bias=quarter_turn[:]
-    )
-    nc.scalar.activation(out=tables[:, :, 0, :], in_=emb[:], func=ACT.Sin, bias=quarter_turn[:])
-    nc.scalar.activation(out=tables[:, :, 1, 0:HALF], in_=emb[:, :, 0:HALF], func=ACT.Sin, scale=-1.0)
-    nc.scalar.activation(out=tables[:, :, 1, HALF:E], in_=emb[:, :, HALF:E], func=ACT.Sin)
 
 
 def tile_rotaryembeddingtransformerlayer_pa_t_kernel(
@@ -76,28 +49,40 @@ def tile_rotaryembeddingtransformerlayer_pa_t_kernel(
         tc.tile_pool(name="xin", bufs=3) as xin,
         tc.tile_pool(name="small", bufs=3) as small,
         tc.tile_pool(name="norm", bufs=2) as norm,
-        tc.tile_pool(name="planes", bufs=1) as plane_pool,
+        tc.tile_pool(name="planes", bufs=2) as plane_pool,
         tc.tile_pool(name="quant", bufs=2) as quant,
         tc.tile_pool(name="mix", bufs=2) as mix,
+        tc.tile_pool(name="outs", bufs=4) as outs,
         tc.psum_pool(name="psum_t", bufs=T_BANKS) as psum_t,
         tc.psum_pool(name="psum_acc", bufs=3) as psum_acc,
-        tc.psum_pool(name="psum_tab", bufs=1) as psum_tab,
+        tc.psum_pool(name="psum_o", bufs=2) as psum_o,
         tc.manual_schedule(),
     ):
-        ident_f32 = const.tile([P, P], F32)
+        ident = const.tile([P, P], F32)
+        evens_odds = const.tile([P, P], F32)
         minus_half = const.tile([P, BATCH], F32)
+        quarter_turn = const.tile([P, 1], F32)
+        parity_sign = const.tile([P, 1], F32)
+        warm = const.tile([P, 1], F32)
         gain = const.tile([P, 2 * CHUNKS], F32)
-        bias_all = const.tile([P, N_OUT], BF16)
+        bias_col = const.tile([P, PACK], F32)
+        bias_v = const.tile([P, E], BF16)
         w_codes = const.tile([P, PASSES, N_OUT], U32, align_bytes=64)
         w_scales = const.tile([P, PASSES, N_OUT], U8, align_bytes=64)
-        tables = const.tile([P, ROUNDS, 2, E], F32)
+        cos_tab = const.tile([P, 2, SEQ], F32)
+        sin_tab = const.tile([P, 2, 2, SEQ], F32)
         w_rows = work.tile([P, N_OUT // P, D], BF16)
         g1_bf16 = work.tile([P, PASSES, PACK], BF16)
         be1_bf16 = work.tile([P, PASSES, PACK], BF16)
+        bias_rows = work.tile([P, P], BF16)
+        bias_rows_f32 = work.tile([P, P], F32)
+        turns = work.tile([P, ROUNDS, HALF], F32)
+        minus_f = work.tile([P, ROUNDS, HALF], F32)
+        emb = work.tile([P, ROUNDS, 2, HALF], F32)
+        emb_pairs = work.tile([P, ROUNDS, HALF, 2], F32)
 
         x_of, moments_of, rstd_of, shift_of, z_of, zT_of = {}, {}, {}, {}, {}, {}
-        planes_of, grouped_of, codes_of, scales_of = {}, {}, {}, {}
-        qk_of, straight_of, turned_of = {}, {}, {}
+        planes_of, grouped_of, codes_of, scales_of, terms_of = {}, {}, {}, {}, {}
 
         def live(t):
             return 0 <= t < ROUNDS
@@ -107,59 +92,116 @@ def tile_rotaryembeddingtransformerlayer_pa_t_kernel(
 
         def load(t):
             x_of[t] = xin.tile([P, BATCH, D], BF16, name="x")
-            nc.sync.dma_start(out=x_of[t][:], in_=src[:, rows(t), :].rearrange("b p k -> p b k"))
+            if t == 0:
+                for b in range(BATCH):
+                    nc.sync.dma_start(out=x_of[t][:, b, :], in_=src[b, rows(t), :])
+            else:
+                nc.sync.dma_start(out=x_of[t][:], in_=src[:, rows(t), :].rearrange("b p k -> p b k"))
 
-        def statistics(t):
-            x = x_of[t]
-            stats = small.tile([P, BATCH, D // BN_CHUNK, 6], F32, name="stats")
-            mean_var = small.tile([P, BATCH, 2], F32, name="mean_var")
-            for b in range(BATCH):
-                for h in range(D // BN_CHUNK):
-                    nc.vector.bn_stats(out=stats[:, b, h, :], in_=x[:, b, h * BN_CHUNK : (h + 1) * BN_CHUNK])
-            for b in range(BATCH):
-                nc.vector.bn_aggr(out=mean_var[:, b, :], in_=stats[:, b, :, :].rearrange("p h s -> p (h s)"))
-            moments_of[t] = mean_var
-
-        def scale_and_shift(t):
-            var_eps = small.tile([P, BATCH], F32, name="var_eps")
+        def table_angles():
+            position_int = work.tile([P, ROUNDS, 1], I32)
+            position = work.tile([P, ROUNDS, 1], F32)
+            nc.gpsimd.iota(position_int[:], pattern=[[P, ROUNDS]], base=0, channel_multiplier=1)
+            nc.vector.tensor_copy(out=position[:], in_=position_int[:])
             nc.gpsimd.tensor_scalar(
-                out=var_eps[:], in0=moments_of[t][:, :, 1], scalar1=1.0, scalar2=EPS, op0=ALU.mult, op1=ALU.add
+                out=turns[:, :, 0:1], in0=position[:], scalar1=0.5 / math.pi, scalar2=0.0, op0=ALU.mult, op1=ALU.add
             )
-            minus_mean = small.tile([P, BATCH], F32, name="minus_mean")
-            nc.gpsimd.tensor_scalar(
-                out=minus_mean[:], in0=moments_of[t][:, :, 0], scalar1=-1.0, scalar2=0.0, op0=ALU.mult, op1=ALU.add
-            )
-            rstd_of[t] = small.tile([P, BATCH], F32, name="rstd")
-            nc.gpsimd.tensor_tensor(out=rstd_of[t][:], in0=var_eps[:], in1=minus_half[:], op=ALU.pow)
-            shift_of[t] = small.tile([P, BATCH], F32, name="shift")
-            nc.gpsimd.tensor_tensor(out=shift_of[t][:], in0=minus_mean[:], in1=rstd_of[t][:], op=ALU.mult)
-
-        def by_chunk(z):
-            return z.rearrange("p (c j m) -> p c j m", c=PASSES, j=PACK)
-
-        def by_slot(x):
-            return x.rearrange("p (c m j) -> p c j m", c=PASSES, j=PACK)
-
-        def normalise_last(t):
-            z_of[t] = norm.tile([P, BATCH, D], F32, name="z")
-            b = BATCH - 1
-            nc.gpsimd.tensor_scalar(
-                out=by_chunk(z_of[t][:, b, :]), in0=by_slot(x_of[t][:, b, :]), scalar1=rstd_of[t][:, b : b + 1],
-                scalar2=shift_of[t][:, b : b + 1], op0=ALU.mult, op1=ALU.add,
-            )
-
-        def normalise(t):
-            for b in range(BATCH - 1):
-                nc.scalar.activation(
-                    out=by_chunk(z_of[t][:, b, :]), in_=by_slot(x_of[t][:, b, :]), func=ACT.Identity,
-                    scale=rstd_of[t][:, b : b + 1], bias=shift_of[t][:, b : b + 1],
+            for doubling in range(7):
+                n = 2**doubling
+                nc.gpsimd.tensor_scalar(
+                    out=turns[:, :, n : 2 * n], in0=turns[:, :, 0:n], scalar1=FREQ_RATIO**n, scalar2=0.0,
+                    op0=ALU.mult, op1=ALU.add,
                 )
+
+        def table_fractions():
+            nc.vector.tensor_scalar(out=minus_f[:], in0=turns[:], scalar1=ROUND_MAGIC, scalar2=None, op0=ALU.add)
+            nc.vector.scalar_tensor_tensor(
+                out=minus_f[:], in0=minus_f[:], scalar=ROUND_MAGIC, in1=turns[:], op0=ALU.subtract, op1=ALU.subtract
+            )
+
+        def table_embedding():
+            nc.scalar.activation(out=emb[:, :, 0, :], in_=minus_f[:], func=ACT.Sin, scale=-2.0 * math.pi)
+            nc.scalar.activation(out=minus_f[:], in_=minus_f[:], func=ACT.Abs)
+            nc.scalar.activation(
+                out=emb[:, :, 1, :], in_=minus_f[:], func=ACT.Sin, scale=-2.0 * math.pi, bias=quarter_turn[:]
+            )
+            nc.gpsimd.tensor_scalar(
+                out=emb_pairs[:], in0=emb[:].rearrange("p t s i -> p t i s"), scalar1=1.0, scalar2=0.0,
+                op0=ALU.mult, op1=ALU.add,
+            )
+
+        def table_part(h, g):
+            cols = slice(BANK * g, BANK * (g + 1))
+            straight = psum_o.tile([P, BANK], F32, name="table", tag="o")
+            for r in range(4):
+                nc.tensor.transpose(straight[:, r * P : (r + 1) * P], emb[:, 4 * g + r, h, :], ident[:])
+            nc.scalar.activation(out=cos_tab[:, h, cols], in_=straight[:], func=ACT.Sin, bias=quarter_turn[:])
+            turned = psum_o.tile([P, BANK], F32, name="table", tag="o")
+            for r in range(4):
+                nc.tensor.transpose(
+                    turned[:, r * P : (r + 1) * P],
+                    emb_pairs[:, 4 * g + r, 64 * h : 64 * (h + 1), :].rearrange("p i s -> p (i s)"),
+                    ident[:],
+                )
+            nc.scalar.activation(out=sin_tab[:, 0, h, cols], in_=turned[:], func=ACT.Sin, scale=parity_sign[:])
+            nc.gpsimd.tensor_scalar(
+                out=sin_tab[:, 1, h, cols], in0=sin_tab[:, 0, h, cols], scalar1=-1.0, scalar2=0.0,
+                op0=ALU.mult, op1=ALU.add,
+            )
+
+        def bn(t, b):
+            if b == 0:
+                moments_of[t] = (
+                    small.tile([P, BATCH, D // BN_CHUNK, 6], F32, name="stats"),
+                    small.tile([P, BATCH, 2], F32, name="mean_var"),
+                )
+            for h in range(D // BN_CHUNK):
+                nc.vector.bn_stats(
+                    out=moments_of[t][0][:, b, h, :], in_=x_of[t][:, b, h * BN_CHUNK : (h + 1) * BN_CHUNK]
+                )
+
+        def aggregate(t, b):
+            nc.vector.bn_aggr(
+                out=moments_of[t][1][:, b, :], in_=moments_of[t][0][:, b, :, :].rearrange("p h s -> p (h s)")
+            )
+
+        def scale_and_shift(t, lo, hi):
+            n = hi - lo
+            mean_var = moments_of[t][1]
+            var_eps = small.tile([P, BATCH], F32, name="var_eps")
+            minus_mean = small.tile([P, BATCH], F32, name="minus_mean")
+            if lo == 0:
+                rstd_of[t] = small.tile([P, BATCH], F32, name="rstd")
+                shift_of[t] = small.tile([P, BATCH], F32, name="shift")
+            nc.gpsimd.tensor_scalar(
+                out=var_eps[:, 0:n], in0=mean_var[:, lo:hi, 1], scalar1=1.0, scalar2=EPS, op0=ALU.mult, op1=ALU.add
+            )
+            nc.gpsimd.tensor_scalar(
+                out=minus_mean[:, 0:n], in0=mean_var[:, lo:hi, 0], scalar1=-1.0, scalar2=0.0, op0=ALU.mult, op1=ALU.add
+            )
+            nc.gpsimd.tensor_tensor(
+                out=rstd_of[t][:, lo:hi], in0=var_eps[:, 0:n], in1=minus_half[:, 0:n], op=ALU.pow
+            )
+            nc.gpsimd.tensor_tensor(
+                out=shift_of[t][:, lo:hi], in0=minus_mean[:, 0:n], in1=rstd_of[t][:, lo:hi], op=ALU.mult
+            )
+
+        def normalise(t, b, on_gpsimd):
+            if b == 0:
+                z_of[t] = norm.tile([P, BATCH, D], F32, name="z")
+            out = z_of[t][:, b, :].rearrange("p (c j m) -> p c j m", c=PASSES, j=PACK)
+            x = x_of[t][:, b, :].rearrange("p (c m j) -> p c j m", c=PASSES, j=PACK)
+            rstd, shift = rstd_of[t][:, b : b + 1], shift_of[t][:, b : b + 1]
+            if on_gpsimd:
+                nc.gpsimd.tensor_scalar(out=out, in0=x, scalar1=rstd, scalar2=shift, op0=ALU.mult, op1=ALU.add)
+            else:
+                nc.scalar.activation(out=out, in_=x, func=ACT.Identity, scale=rstd, bias=shift)
 
         def transpose(t, kc):
             zT_of[t, kc] = psum_t.tile([P, TOKENS], F32, name="zT")
             for b in range(BATCH):
                 nc.tensor.transpose(
-                    zT_of[t, kc][:, b * P : (b + 1) * P], z_of[t][:, b, kc * P : (kc + 1) * P], ident_f32[:]
+                    zT_of[t, kc][:, b * P : (b + 1) * P], z_of[t][:, b, kc * P : (kc + 1) * P], ident[:]
                 )
 
         def gain_out(t, kc):
@@ -170,13 +212,20 @@ def tile_rotaryembeddingtransformerlayer_pa_t_kernel(
                 scale=gain[:, kc : kc + 1], bias=gain[:, CHUNKS + kc : CHUNKS + kc + 1],
             )
 
-        def regroup(t, c):
+        def regroup(t, c, on_gpsimd):
             if c == 0:
                 grouped_of[t] = quant.tile([P, PASSES, TOKENS, PACK], BF16, name="grouped", align_bytes=64)
-            nc.scalar.copy(
-                out=grouped_of[t][:, c, :, :].rearrange("p (m i) j -> p m j i", i=4),
-                in_=planes_of[t][:, PACK * c : PACK * (c + 1), :].rearrange("p j (m i) -> p m j i", i=4),
-            )
+            out = grouped_of[t][:, c, :, :]
+            planes = planes_of[t][:, PACK * c : PACK * (c + 1), :]
+            if on_gpsimd:
+                nc.gpsimd.tensor_scalar(
+                    out=out, in0=planes.rearrange("p j m -> p m j"), scalar1=1.0, scalar2=0.0,
+                    op0=ALU.mult, op1=ALU.add,
+                )
+            else:
+                nc.scalar.copy(
+                    out=out.rearrange("p (m i) j -> p m j i", i=4), in_=planes.rearrange("p j (m i) -> p m j i", i=4)
+                )
 
         def quantise(t):
             codes_of[t] = quant.tile([P, PASSES, TOKENS], U32, name="codes", align_bytes=64)
@@ -187,141 +236,210 @@ def tile_rotaryembeddingtransformerlayer_pa_t_kernel(
                 in_=grouped_of[t][:].rearrange("p c w j -> p (c w j)"),
             )
 
-        def multiply(acc, t, b, lo, hi):
-            tok = slice(b * P, (b + 1) * P)
+        def multiply_qk(t, n):
+            acc = psum_acc.tile([P, BANK], F32, name="acc", tag="acc")
+            cols = slice(n * P, (n + 1) * P)
             for c in range(PASSES):
                 nc.tensor.matmul_mx(
-                    out=acc,
-                    lhsT=codes_of[t][:, c, tok].bitcast(FP8X4), lhsT_scale=scales_of[t][:, c, tok],
-                    rhs=w_codes[:, c, lo:hi].bitcast(FP8X4), rhs_scale=w_scales[:, c, lo:hi],
+                    out=acc[:],
+                    lhsT=w_codes[:, c, cols].bitcast(FP8X4), lhsT_scale=w_scales[:, c, cols],
+                    rhs=codes_of[t][:, c, :].bitcast(FP8X4), rhs_scale=scales_of[t][:, c, :],
                     start=(c == 0), stop=(c == PASSES - 1),
                 )
+            return acc
 
-        def turn(engine, t, pair, sines):
-            engine.tensor_tensor(
-                out=turned_of[t][:, pair].rearrange("p b q (h i) -> p (b q) h i", h=2),
-                in0=qk_of[t][:, pair].rearrange("p b q (i h) -> p (b q) h i", h=2),
-                in1=sines.rearrange("p (h i) -> p h i", h=2).unsqueeze(1).to_broadcast([P, 4, 2, HALF]),
-                op=ALU.mult,
-            )
-
-        def project(t):
-            tab_ps = psum_tab.tile([P, 2, E], F32, name="tab_ps")
-            nc.tensor.matmul(
-                out=tab_ps[:].rearrange("p s e -> p (s e)"), lhsT=ident_f32[:],
-                rhs=tables[:, t, :, :].rearrange("p s e -> p (s e)"), start=True, stop=True,
-            )
-            qk_of[t] = mix.tile([P, BATCH, 2, E], F32, name="qk")
-            straight_of[t] = mix.tile([P, BATCH, 2, E], F32, name="straight")
-            turned_of[t] = mix.tile([P, BATCH, 2, E], F32, name="turned")
-            v = mix.tile([P, BATCH, E], F32, name="v")
-            for b in range(BATCH):
-                acc_qk = psum_acc.tile([P, 2 * E], F32, name="acc_qk", tag="acc")
-                multiply(acc_qk[:], t, b, 0, 2 * E)
-                nc.vector.tensor_tensor(
-                    out=qk_of[t][:, b, :, :].rearrange("p q e -> p (q e)"), in0=acc_qk[:],
-                    in1=bias_all[:, 0 : 2 * E], op=ALU.add,
+        def mix_terms(t, n, acc):
+            qk, h = divmod(n, 2)
+            if h == 0:
+                terms_of[t, qk] = mix.tile([P, 2, 2, BATCH, P], F32, name="terms")
+            for term, table in ((0, cos_tab[:, h, rows(t)]), (1, sin_tab[:, qk, h, rows(t)])):
+                nc.vector.scalar_tensor_tensor(
+                    out=terms_of[t, qk][:, term, h], in0=acc[:].rearrange("p (b s) -> p b s", b=BATCH),
+                    scalar=bias_col[:, n : n + 1], in1=table.unsqueeze(1).to_broadcast([P, BATCH, P]),
+                    op0=ALU.add, op1=ALU.mult,
                 )
-                if b % 2 == 0:
-                    acc_v = psum_acc.tile([P, 2, E], F32, name="acc_v", tag="acc")
-                multiply(acc_v[:, b % 2, :], t, b, 2 * E, N_OUT)
-                if b % 2 == 1:
-                    pair = slice(b - 1, b + 1)
-                    nc.vector.tensor_tensor(
-                        out=v[:, pair, :], in0=acc_v[:],
-                        in1=bias_all[:, 2 * E : N_OUT].unsqueeze(1).to_broadcast([P, 2, E]), op=ALU.add,
-                    )
-                    nc.vector.tensor_tensor(
-                        out=straight_of[t][:, pair].rearrange("p b q e -> p (b q) e"),
-                        in0=qk_of[t][:, pair].rearrange("p b q e -> p (b q) e"),
-                        in1=tab_ps[:, 0, :].unsqueeze(1).to_broadcast([P, 4, E]),
-                        op=ALU.mult,
-                    )
-            turn(nc.vector, t, slice(2, 4), tab_ps[:, 1, :])
-            nc.sync.dma_start(out=out_2[:, rows(t), :].rearrange("b p e -> p b e"), in_=v[:])
 
-        def finish_mix(t):
-            straight, turned = straight_of[t], turned_of[t]
-            turn(nc.gpsimd, t, slice(0, 2), tables[:, t, 1, :])
-            for b in range(0, BATCH, 2):
-                pair = slice(b, b + 2)
-                for q, out, op in ((0, out_0, ALU.add), (1, out_1, ALU.subtract)):
-                    nc.gpsimd.tensor_tensor(
-                        out=straight[:, pair, q, :], in0=straight[:, pair, q, :], in1=turned[:, pair, q, :], op=op
+        def mix_back(t, qk, b0):
+            terms = terms_of[t, qk]
+            total = psum_o.tile([P, 2, E], F32, name="total", tag="o")
+            for b in range(2):
+                for h in range(2):
+                    nc.tensor.matmul(
+                        out=total[:, b, h * P : (h + 1) * P], lhsT=terms[:, 0, h, b0 + b, :], rhs=ident[:],
+                        start=(h == 0), stop=False, is_transpose=True,
                     )
-                    nc.sync.dma_start(
-                        out=out[pair, rows(t), :].rearrange("b p e -> p b e"), in_=straight[:, pair, q, :]
+                for h in range(2):
+                    nc.tensor.matmul(
+                        out=total[:, b, :].rearrange("p (s m g) -> p m s g", s=2, m=2)[:, h],
+                        lhsT=terms[:, 1, h, b0 + b, :], rhs=evens_odds[:],
+                        start=False, stop=(h == 1), is_transpose=True,
                     )
+            return total
 
-        def prepare_gain():
+        def mix_out(t, qk, b0, total):
+            result = outs.tile([P, 2, E], F32, name="result")
+            nc.scalar.copy(out=result[:], in_=total[:])
+            out = (out_0, out_1)[qk]
+            nc.sync.dma_start(out=out[b0 : b0 + 2, rows(t), :].rearrange("b p e -> p b e"), in_=result[:])
+
+        def multiply_v(t, b0):
+            acc = psum_acc.tile([P, 2, E], F32, name="acc_v", tag="acc")
+            for b in range(2):
+                tok = slice((b0 + b) * P, (b0 + b + 1) * P)
+                for c in range(PASSES):
+                    nc.tensor.matmul_mx(
+                        out=acc[:, b, :],
+                        lhsT=codes_of[t][:, c, tok].bitcast(FP8X4), lhsT_scale=scales_of[t][:, c, tok],
+                        rhs=w_codes[:, c, 2 * E : N_OUT].bitcast(FP8X4), rhs_scale=w_scales[:, c, 2 * E : N_OUT],
+                        start=(c == 0), stop=(c == PASSES - 1),
+                    )
+            return acc
+
+        def add_bias_v(t, b0, acc):
+            v = outs.tile([P, 2, E], F32, name="v")
+            nc.vector.tensor_tensor(
+                out=v[:], in0=acc[:], in1=bias_v[:].unsqueeze(1).to_broadcast([P, 2, E]), op=ALU.add
+            )
+            nc.sync.dma_start(out=out_2[b0 : b0 + 2, rows(t), :].rearrange("b p e -> p b e"), in_=v[:])
+
+        def prepare_constants():
             nc.vector.tensor_copy(out=gain[:, 0:CHUNKS], in_=g1_bf16[:].rearrange("p c j -> p (c j)"))
             nc.vector.tensor_copy(out=gain[:, CHUNKS : 2 * CHUNKS], in_=be1_bf16[:].rearrange("p c j -> p (c j)"))
+            nc.vector.tensor_copy(out=bias_rows_f32[:], in_=bias_rows[:])
+            bias_ps = psum_o.tile([P, P], F32, name="bias_ps", tag="o")
+            nc.tensor.transpose(bias_ps[:], bias_rows_f32[:], ident[:])
+            nc.vector.tensor_copy(out=bias_col[:], in_=bias_ps[:, 0:PACK])
+            nc.vector.tensor_copy(
+                out=evens_odds[:].rearrange("p (s g) -> p s g", s=2), in_=ident[:].rearrange("p (g s) -> p s g", s=2)
+            )
+            nc.vector.reduce_sum(out=parity_sign[:], in_=ident[:, 0:P:2], axis=AX.X)
+            nc.vector.tensor_scalar(
+                out=parity_sign[:], in0=parity_sign[:], scalar1=-2.0, scalar2=1.0, op0=ALU.mult, op1=ALU.add
+            )
 
-        def prepare_weights():
+        w_grouped = work.tile([P, PASSES, N_OUT, PACK], BF16, name="w_grouped", align_bytes=64)
+
+        def weights_turn(c, pair):
             w_words = w_rows[:].rearrange("p r k -> p (r k)").bitcast(F32).rearrange("p (r w) -> p r w", r=N_OUT // P)
-            w_grouped = work.tile([P, PASSES, N_OUT, PACK], BF16, name="w_grouped", align_bytes=64)
-            for c in range(PASSES):
-                for pair in range(N_OUT // (2 * P)):
-                    wT = psum_acc.tile([P, 2, 2 * P], F32, name="wT", tag="acc")
-                    for u in range(2):
-                        for h in range(2):
-                            nc.tensor.transpose(
-                                wT[:, u, h * P : (h + 1) * P],
-                                w_words[:, 2 * pair + h, 2 * P * c + u : 2 * P * (c + 1) : 2],
-                                ident_f32[:],
-                            )
-                    nc.vector.tensor_copy(
-                        out=w_grouped[:, c, 2 * P * pair : 2 * P * (pair + 1), :]
-                        .rearrange("p n j -> p (n j)").bitcast(F32).rearrange("p (n u) -> p n u", u=2),
-                        in_=wT[:].rearrange("p u n -> p n u"),
+            wT = psum_acc.tile([P, 2, 2 * P], F32, name="wT", tag="acc")
+            for u in range(2):
+                for h in range(2):
+                    nc.tensor.transpose(
+                        wT[:, u, h * P : (h + 1) * P],
+                        w_words[:, 2 * pair + h, 2 * P * c + u : 2 * P * (c + 1) : 2],
+                        ident[:],
                     )
-            for c in range(PASSES):
-                for lo, hi in ((0, 2 * E), (2 * E, N_OUT)):
-                    nc.vector.quantize_mx(
-                        out=w_codes[:, c, lo:hi].bitcast(FP8X4),
-                        scales=w_scales[:, c, lo:hi],
-                        in_=w_grouped[:, c, lo:hi, :].rearrange("p n j -> p (n j)"),
-                    )
+            nc.vector.tensor_copy(
+                out=w_grouped[:, c, 2 * P * pair : 2 * P * (pair + 1), :]
+                .rearrange("p n j -> p (n j)").bitcast(F32).rearrange("p (n u) -> p n u", u=2),
+                in_=wT[:].rearrange("p u n -> p n u"),
+            )
+
+        def weights_quantise(c):
+            for lo, hi in ((0, 2 * E), (2 * E, N_OUT)):
+                nc.vector.quantize_mx(
+                    out=w_codes[:, c, lo:hi].bitcast(FP8X4),
+                    scales=w_scales[:, c, lo:hi],
+                    in_=w_grouped[:, c, lo:hi, :].rearrange("p n j -> p (n j)"),
+                )
 
         load(0)
+        nc.vector.memset(bias_rows[:], 0.0)
+        nc.vector.memset(minus_half[:], -0.5)
+        nc.vector.memset(quarter_turn[:], 1.0)
+        nc.vector.tensor_scalar(
+            out=quarter_turn[:], in0=quarter_turn[:], scalar1=0.5 * math.pi, scalar2=None, op0=ALU.mult
+        )
+        nc.scalar.activation(out=warm[:], in_=quarter_turn[:], func=ACT.Sin)
         nc.sync.dma_start(out=g1_bf16[:], in_=g1.rearrange("(c p j) -> p c j", c=PASSES, j=PACK))
         nc.sync.dma_start(out=be1_bf16[:], in_=be1.rearrange("(c p j) -> p c j", c=PASSES, j=PACK))
+        nc.sync.dma_start(out=bias_rows[0:PACK, :], in_=bqkv[0 : 2 * E].rearrange("(r p) -> r p", p=P))
         load(1)
         nc.sync.dma_start(out=w_rows[:], in_=Wqkv.rearrange("(r p) k -> p r k", p=P))
-        nc.sync.dma_start(out=bias_all[:], in_=bqkv.partition_broadcast(P))
+        nc.sync.dma_start(out=bias_v[:], in_=bqkv[2 * E : N_OUT].partition_broadcast(P))
         load(2)
-        make_identity(nc, ident_f32[:])
-        nc.vector.memset(minus_half[:], -0.5)
-        build_position_tables(nc, work, tables)
-        prepare_gain()
+        table_angles()
+        make_identity(nc, ident[:])
+        for b0 in (0, 2):
+            for b in (b0, b0 + 1):
+                bn(0, b)
+            for b in (b0, b0 + 1):
+                aggregate(0, b)
+            scale_and_shift(0, b0, b0 + 2)
+            normalise(0, b0, True)
+            normalise(0, b0 + 1, False)
+        prepare_constants()
+        table_fractions()
+        for kc in range(T_BANKS):
+            transpose(0, kc)
+        for b in range(BATCH):
+            bn(1, b)
+        for b in range(BATCH):
+            aggregate(1, b)
+        scale_and_shift(1, 0, BATCH)
 
-        for i in range(-2, ROUNDS + 1):
-            if live(i + 3) and i >= 0:
+        for i in range(0, ROUNDS + 1):
+            if live(i + 3):
                 load(i + 3)
-            if live(i - 1):
-                quantise(i - 1)
             if live(i):
-                for kc in range(CHUNKS - T_BANKS):
+                for kc in range(CHUNKS - 2 - T_BANKS):
                     gain_out(i, kc)
                     transpose(i, kc + T_BANKS)
-            if live(i + 2):
-                statistics(i + 2)
             if i == 0:
-                prepare_weights()
+                table_embedding()
+                for c in range(PASSES):
+                    for pair in range(N_OUT // (2 * P)):
+                        weights_turn(c, pair)
+                for c in range(PASSES):
+                    weights_quantise(c)
+            accs = {}
             if live(i - 1):
-                project(i - 1)
-            if live(i):
-                for kc in range(CHUNKS - T_BANKS, CHUNKS):
-                    gain_out(i, kc)
+                quantise(i - 1)
+            if live(i + 2):
+                bn(i + 2, 0)
+            if live(i - 1):
+                for n in (0, 1):
+                    accs[n] = multiply_qk(i - 1, n)
+                for n in (0, 1):
+                    mix_terms(i - 1, n, accs[n])
             if live(i + 1):
-                normalise(i + 1)
+                for b in range(G_NORM):
+                    normalise(i + 1, b, True)
+            if live(i):
+                gain_out(i, 3)
+                regroup(i, 0, True)
+                transpose(i, 6)
+                gain_out(i, 4)
+                transpose(i, 7)
+                for kc in range(5, CHUNKS):
+                    gain_out(i, kc)
+            if i in (0, 1):
+                for h in range(2):
+                    table_part(h, i)
+            if live(i):
+                regroup(i, 1, False)
+            if live(i - 1):
+                for n in (2, 3):
+                    accs[n] = multiply_qk(i - 1, n)
+                for n in (2, 3):
+                    mix_terms(i - 1, n, accs[n])
+                for b0 in (0, 2):
+                    mix_out(i - 1, 0, b0, mix_back(i - 1, 0, b0))
+                for b0 in (0, 2):
+                    add_bias_v(i - 1, b0, multiply_v(i - 1, b0))
+            if live(i + 2):
+                for b in range(1, BATCH):
+                    bn(i + 2, b)
+                for b in range(BATCH):
+                    aggregate(i + 2, b)
+            if live(i + 1):
+                for b in range(G_NORM, BATCH):
+                    normalise(i + 1, b, False)
+            if live(i - 1):
+                for b0 in (0, 2):
+                    mix_out(i - 1, 1, b0, mix_back(i - 1, 1, b0))
+            if live(i + 1):
                 for kc in range(T_BANKS):
                     transpose(i + 1, kc)
             if live(i + 2):
-                scale_and_shift(i + 2)
-                normalise_last(i + 2)
-            if live(i - 1):
-                finish_mix(i - 1)
-            if live(i):
-                regroup(i, 0)
-                regroup(i, 1)
+                scale_and_shift(i + 2, 0, BATCH)

@@ -31,7 +31,7 @@ TOKENS = BATCH * P
 BN_CHUNK = 512
 BANK = 512
 T_BANKS = 3
-G_NORM = 4
+S_NORM = 3
 
 FREQ_RATIO = 10000.0 ** (-1.0 / HALF)
 ROUND_MAGIC = 12582912.0
@@ -51,7 +51,7 @@ def tile_rotaryembeddingtransformerlayer_pa_t_kernel(
         tc.tile_pool(name="norm", bufs=2) as norm,
         tc.tile_pool(name="planes", bufs=2) as plane_pool,
         tc.tile_pool(name="quant", bufs=2) as quant,
-        tc.tile_pool(name="mix", bufs=2) as mix,
+        tc.tile_pool(name="mix", bufs=3) as mix,
         tc.tile_pool(name="outs", bufs=4) as outs,
         tc.psum_pool(name="psum_t", bufs=T_BANKS) as psum_t,
         tc.psum_pool(name="psum_acc", bufs=3) as psum_acc,
@@ -99,54 +99,62 @@ def tile_rotaryembeddingtransformerlayer_pa_t_kernel(
                 nc.sync.dma_start(out=x_of[t][:], in_=src[:, rows(t), :].rearrange("b p k -> p b k"))
 
         def table_angles():
-            position_int = work.tile([P, ROUNDS, 1], I32)
-            position = work.tile([P, ROUNDS, 1], F32)
-            nc.gpsimd.iota(position_int[:], pattern=[[P, ROUNDS]], base=0, channel_multiplier=1)
-            nc.vector.tensor_copy(out=position[:], in_=position_int[:])
-            nc.gpsimd.tensor_scalar(
-                out=turns[:, :, 0:1], in0=position[:], scalar1=0.5 / math.pi, scalar2=0.0, op0=ALU.mult, op1=ALU.add
+            position = work.tile([P, ROUNDS, 1], I32)
+            nc.gpsimd.iota(position[:], pattern=[[P, ROUNDS]], base=0, channel_multiplier=1)
+            nc.vector.tensor_scalar(
+                out=turns[:, :, 0:1], in0=position[:], scalar1=0.5 / math.pi, scalar2=None, op0=ALU.mult
             )
             for doubling in range(7):
                 n = 2**doubling
-                nc.gpsimd.tensor_scalar(
-                    out=turns[:, :, n : 2 * n], in0=turns[:, :, 0:n], scalar1=FREQ_RATIO**n, scalar2=0.0,
-                    op0=ALU.mult, op1=ALU.add,
+                nc.vector.tensor_scalar(
+                    out=turns[:, :, n : 2 * n], in0=turns[:, :, 0:n], scalar1=FREQ_RATIO**n, scalar2=None, op0=ALU.mult
                 )
 
-        def table_fractions():
-            nc.vector.tensor_scalar(out=minus_f[:], in0=turns[:], scalar1=ROUND_MAGIC, scalar2=None, op0=ALU.add)
+        def table_fractions(g):
+            half = slice(4 * g, 4 * (g + 1))
+            nc.vector.tensor_scalar(
+                out=minus_f[:, half], in0=turns[:, half], scalar1=ROUND_MAGIC, scalar2=None, op0=ALU.add
+            )
             nc.vector.scalar_tensor_tensor(
-                out=minus_f[:], in0=minus_f[:], scalar=ROUND_MAGIC, in1=turns[:], op0=ALU.subtract, op1=ALU.subtract
+                out=minus_f[:, half], in0=minus_f[:, half], scalar=ROUND_MAGIC, in1=turns[:, half],
+                op0=ALU.subtract, op1=ALU.subtract,
             )
 
-        def table_embedding():
-            nc.scalar.activation(out=emb[:, :, 0, :], in_=minus_f[:], func=ACT.Sin, scale=-2.0 * math.pi)
-            nc.scalar.activation(out=minus_f[:], in_=minus_f[:], func=ACT.Abs)
+        def table_embedding(g):
+            half = slice(4 * g, 4 * (g + 1))
+            nc.scalar.activation(out=emb[:, half, 0, :], in_=minus_f[:, half], func=ACT.Sin, scale=-2.0 * math.pi)
+            nc.scalar.activation(out=minus_f[:, half], in_=minus_f[:, half], func=ACT.Abs)
             nc.scalar.activation(
-                out=emb[:, :, 1, :], in_=minus_f[:], func=ACT.Sin, scale=-2.0 * math.pi, bias=quarter_turn[:]
+                out=emb[:, half, 1, :], in_=minus_f[:, half], func=ACT.Sin, scale=-2.0 * math.pi, bias=quarter_turn[:]
             )
             nc.gpsimd.tensor_scalar(
-                out=emb_pairs[:], in0=emb[:].rearrange("p t s i -> p t i s"), scalar1=1.0, scalar2=0.0,
+                out=emb_pairs[:, half], in0=emb[:, half].rearrange("p t s i -> p t i s"), scalar1=1.0, scalar2=0.0,
                 op0=ALU.mult, op1=ALU.add,
             )
 
-        def table_part(h, g):
-            cols = slice(BANK * g, BANK * (g + 1))
-            straight = psum_o.tile([P, BANK], F32, name="table", tag="o")
+        def table_cos(h, g):
+            angle = psum_o.tile([P, BANK], F32, name="angle", tag="o")
             for r in range(4):
-                nc.tensor.transpose(straight[:, r * P : (r + 1) * P], emb[:, 4 * g + r, h, :], ident[:])
-            nc.scalar.activation(out=cos_tab[:, h, cols], in_=straight[:], func=ACT.Sin, bias=quarter_turn[:])
-            turned = psum_o.tile([P, BANK], F32, name="table", tag="o")
+                nc.tensor.transpose(angle[:, r * P : (r + 1) * P], emb[:, 4 * g + r, h, :], ident[:])
+            nc.scalar.activation(
+                out=cos_tab[:, h, BANK * g : BANK * (g + 1)], in_=angle[:], func=ACT.Sin, bias=quarter_turn[:]
+            )
+
+        def table_sin(h, g):
+            angle = psum_o.tile([P, BANK], F32, name="angle", tag="o")
             for r in range(4):
                 nc.tensor.transpose(
-                    turned[:, r * P : (r + 1) * P],
+                    angle[:, r * P : (r + 1) * P],
                     emb_pairs[:, 4 * g + r, 64 * h : 64 * (h + 1), :].rearrange("p i s -> p (i s)"),
                     ident[:],
                 )
-            nc.scalar.activation(out=sin_tab[:, 0, h, cols], in_=turned[:], func=ACT.Sin, scale=parity_sign[:])
+            nc.scalar.activation(
+                out=sin_tab[:, 0, h, BANK * g : BANK * (g + 1)], in_=angle[:], func=ACT.Sin, scale=parity_sign[:]
+            )
+
+        def table_negate():
             nc.gpsimd.tensor_scalar(
-                out=sin_tab[:, 1, h, cols], in0=sin_tab[:, 0, h, cols], scalar1=-1.0, scalar2=0.0,
-                op0=ALU.mult, op1=ALU.add,
+                out=sin_tab[:, 1], in0=sin_tab[:, 0], scalar1=-1.0, scalar2=0.0, op0=ALU.mult, op1=ALU.add
             )
 
         def bn(t, b):
@@ -164,6 +172,13 @@ def tile_rotaryembeddingtransformerlayer_pa_t_kernel(
             nc.vector.bn_aggr(
                 out=moments_of[t][1][:, b, :], in_=moments_of[t][0][:, b, :, :].rearrange("p h s -> p (h s)")
             )
+
+        def moments(t):
+            for b in range(BATCH):
+                bn(t, b)
+            for b in range(BATCH):
+                aggregate(t, b)
+            scale_and_shift(t, 0, BATCH)
 
         def scale_and_shift(t, lo, hi):
             n = hi - lo
@@ -187,7 +202,7 @@ def tile_rotaryembeddingtransformerlayer_pa_t_kernel(
             )
 
         def normalise(t, b, on_gpsimd):
-            if b == 0:
+            if t not in z_of:
                 z_of[t] = norm.tile([P, BATCH, D], F32, name="z")
             out = z_of[t][:, b, :].rearrange("p (c j m) -> p c j m", c=PASSES, j=PACK)
             x = x_of[t][:, b, :].rearrange("p (c m j) -> p c j m", c=PASSES, j=PACK)
@@ -212,20 +227,14 @@ def tile_rotaryembeddingtransformerlayer_pa_t_kernel(
                 scale=gain[:, kc : kc + 1], bias=gain[:, CHUNKS + kc : CHUNKS + kc + 1],
             )
 
-        def regroup(t, c, on_gpsimd):
+        def regroup(t, c):
             if c == 0:
                 grouped_of[t] = quant.tile([P, PASSES, TOKENS, PACK], BF16, name="grouped", align_bytes=64)
-            out = grouped_of[t][:, c, :, :]
-            planes = planes_of[t][:, PACK * c : PACK * (c + 1), :]
-            if on_gpsimd:
-                nc.gpsimd.tensor_scalar(
-                    out=out, in0=planes.rearrange("p j m -> p m j"), scalar1=1.0, scalar2=0.0,
-                    op0=ALU.mult, op1=ALU.add,
-                )
-            else:
-                nc.scalar.copy(
-                    out=out.rearrange("p (m i) j -> p m j i", i=4), in_=planes.rearrange("p j (m i) -> p m j i", i=4)
-                )
+            nc.gpsimd.tensor_scalar(
+                out=grouped_of[t][:, c, :, :],
+                in0=planes_of[t][:, PACK * c : PACK * (c + 1), :].rearrange("p j m -> p m j"),
+                scalar1=1.0, scalar2=0.0, op0=ALU.mult, op1=ALU.add,
+            )
 
         def quantise(t):
             codes_of[t] = quant.tile([P, PASSES, TOKENS], U32, name="codes", align_bytes=64)
@@ -329,6 +338,9 @@ def tile_rotaryembeddingtransformerlayer_pa_t_kernel(
                         w_words[:, 2 * pair + h, 2 * P * c + u : 2 * P * (c + 1) : 2],
                         ident[:],
                     )
+            return wT
+
+        def weights_copy(c, pair, wT):
             nc.vector.tensor_copy(
                 out=w_grouped[:, c, 2 * P * pair : 2 * P * (pair + 1), :]
                 .rearrange("p n j -> p (n j)").bitcast(F32).rearrange("p (n u) -> p n u", u=2),
@@ -360,6 +372,9 @@ def tile_rotaryembeddingtransformerlayer_pa_t_kernel(
         load(2)
         table_angles()
         make_identity(nc, ident[:])
+        for g in range(2):
+            table_fractions(g)
+            table_embedding(g)
         for b0 in (0, 2):
             for b in (b0, b0 + 1):
                 bn(0, b)
@@ -369,77 +384,76 @@ def tile_rotaryembeddingtransformerlayer_pa_t_kernel(
             normalise(0, b0, True)
             normalise(0, b0 + 1, False)
         prepare_constants()
-        table_fractions()
+        for h in range(2):
+            table_cos(h, 0)
         for kc in range(T_BANKS):
             transpose(0, kc)
-        for b in range(BATCH):
-            bn(1, b)
-        for b in range(BATCH):
-            aggregate(1, b)
-        scale_and_shift(1, 0, BATCH)
+        moments(1)
 
-        for i in range(0, ROUNDS + 1):
-            if live(i + 3):
-                load(i + 3)
-            if live(i):
-                for kc in range(CHUNKS - 2 - T_BANKS):
-                    gain_out(i, kc)
-                    transpose(i, kc + T_BANKS)
-            if i == 0:
-                table_embedding()
-                for c in range(PASSES):
-                    for pair in range(N_OUT // (2 * P)):
-                        weights_turn(c, pair)
+        v_accs, q_sums = [], []
+        for r in range(ROUNDS + 2):
+            m = r - 1
+            if live(r + 3):
+                load(r + 3)
+            for b0, acc in v_accs:
+                add_bias_v(m - 1, b0, acc)
+            v_accs = []
+            if live(r + 2):
+                for b in range(BATCH):
+                    bn(r + 2, b)
+                for b in range(BATCH):
+                    aggregate(r + 2, b)
+            if r == 1:
+                for pair in range(N_OUT // (2 * P)):
+                    weights_copy(1, pair, wTs[pair])
                 for c in range(PASSES):
                     weights_quantise(c)
-            accs = {}
-            if live(i - 1):
-                quantise(i - 1)
-            if live(i + 2):
-                bn(i + 2, 0)
-            if live(i - 1):
-                for n in (0, 1):
-                    accs[n] = multiply_qk(i - 1, n)
-                for n in (0, 1):
-                    mix_terms(i - 1, n, accs[n])
-            if live(i + 1):
-                for b in range(G_NORM):
-                    normalise(i + 1, b, True)
-            if live(i):
-                gain_out(i, 3)
-                regroup(i, 0, True)
-                transpose(i, 6)
-                gain_out(i, 4)
-                transpose(i, 7)
-                for kc in range(5, CHUNKS):
-                    gain_out(i, kc)
-            if i in (0, 1):
-                for h in range(2):
-                    table_part(h, i)
-            if live(i):
-                regroup(i, 1, False)
-            if live(i - 1):
-                for n in (2, 3):
-                    accs[n] = multiply_qk(i - 1, n)
-                for n in (2, 3):
-                    mix_terms(i - 1, n, accs[n])
-                for b0 in (0, 2):
-                    mix_out(i - 1, 0, b0, mix_back(i - 1, 0, b0))
-                for b0 in (0, 2):
-                    add_bias_v(i - 1, b0, multiply_v(i - 1, b0))
-            if live(i + 2):
-                for b in range(1, BATCH):
-                    bn(i + 2, b)
+                quantise(0)
+            if live(r):
+                for kc in range(5):
+                    gain_out(r, kc)
+                    transpose(r, kc + T_BANKS)
+                    if kc == 3:
+                        regroup(r, 0)
+                    if kc == 1 and r == 0:
+                        for pair in range(N_OUT // (2 * P)):
+                            weights_copy(0, pair, weights_turn(0, pair))
+            for args in q_sums:
+                mix_out(*args)
+            if live(m):
+                accs = [multiply_qk(m, n) for n in range(3)]
+                mix_terms(m, 0, accs[0])
+            k_sums = []
+            if live(m - 1):
+                k_sums = [(m - 1, 1, b0, mix_back(m - 1, 1, b0)) for b0 in (0, 2)]
+            if live(m):
+                accs.append(multiply_qk(m, 3))
+                for n in (1, 2, 3):
+                    mix_terms(m, n, accs[n])
+            if live(r + 1):
                 for b in range(BATCH):
-                    aggregate(i + 2, b)
-            if live(i + 1):
-                for b in range(G_NORM, BATCH):
-                    normalise(i + 1, b, False)
-            if live(i - 1):
-                for b0 in (0, 2):
-                    mix_out(i - 1, 1, b0, mix_back(i - 1, 1, b0))
-            if live(i + 1):
+                    normalise(r + 1, b, b >= S_NORM)
+            if live(r + 2):
+                scale_and_shift(r + 2, 0, BATCH)
+            if live(r):
+                for kc in range(5, CHUNKS):
+                    gain_out(r, kc)
+                regroup(r, 1)
+            for args in k_sums:
+                mix_out(*args)
+            if live(r + 1):
                 for kc in range(T_BANKS):
-                    transpose(i + 1, kc)
-            if live(i + 2):
-                scale_and_shift(i + 2, 0, BATCH)
+                    transpose(r + 1, kc)
+            if live(m):
+                v_accs = [(b0, multiply_v(m, b0)) for b0 in (0, 2)]
+                q_sums = [(m, 0, b0, mix_back(m, 0, b0)) for b0 in (0, 2)]
+            if r == 0:
+                wTs = [weights_turn(1, pair) for pair in range(N_OUT // (2 * P))]
+                for h in range(2):
+                    table_sin(h, 0)
+                for h in range(2):
+                    table_cos(h, 1)
+                    table_sin(h, 1)
+                table_negate()
+            if live(r) and r > 0:
+                quantise(r)

@@ -33,6 +33,7 @@ BANK = 512
 T_BANKS = 3
 S_NORM = 3
 
+FIRST_FREQS = 8
 FREQ_RATIO = 10000.0 ** (-1.0 / HALF)
 ROUND_MAGIC = 12582912.0
 
@@ -101,14 +102,17 @@ def tile_rotaryembeddingtransformerlayer_pa_t_kernel(
         def table_angles():
             position = work.tile([P, ROUNDS, 1], I32)
             nc.gpsimd.iota(position[:], pattern=[[P, ROUNDS]], base=0, channel_multiplier=1)
-            nc.vector.tensor_scalar(
-                out=turns[:, :, 0:1], in0=position[:], scalar1=0.5 / math.pi, scalar2=None, op0=ALU.mult
-            )
-            for doubling in range(7):
-                n = 2**doubling
+            for i in range(FIRST_FREQS):
+                nc.vector.tensor_scalar(
+                    out=turns[:, :, i : i + 1], in0=position[:], scalar1=0.5 / math.pi * FREQ_RATIO**i, scalar2=None,
+                    op0=ALU.mult,
+                )
+            n = FIRST_FREQS
+            while n < HALF:
                 nc.vector.tensor_scalar(
                     out=turns[:, :, n : 2 * n], in0=turns[:, :, 0:n], scalar1=FREQ_RATIO**n, scalar2=None, op0=ALU.mult
                 )
+                n *= 2
 
         def table_fractions(g):
             half = slice(4 * g, 4 * (g + 1))
@@ -127,13 +131,16 @@ def tile_rotaryembeddingtransformerlayer_pa_t_kernel(
             nc.scalar.activation(
                 out=emb[:, half, 1, :], in_=minus_f[:, half], func=ACT.Sin, scale=-2.0 * math.pi, bias=quarter_turn[:]
             )
+
+        def table_pairs(g):
+            half = slice(4 * g, 4 * (g + 1))
             nc.gpsimd.tensor_scalar(
                 out=emb_pairs[:, half], in0=emb[:, half].rearrange("p t s i -> p t i s"), scalar1=1.0, scalar2=0.0,
                 op0=ALU.mult, op1=ALU.add,
             )
 
         def table_cos(h, g):
-            angle = psum_o.tile([P, BANK], F32, name="angle", tag="o")
+            angle = psum_t.tile([P, BANK], F32, name="angle", tag="zT")
             for r in range(4):
                 nc.tensor.transpose(angle[:, r * P : (r + 1) * P], emb[:, 4 * g + r, h, :], ident[:])
             nc.scalar.activation(
@@ -141,7 +148,7 @@ def tile_rotaryembeddingtransformerlayer_pa_t_kernel(
             )
 
         def table_sin(h, g):
-            angle = psum_o.tile([P, BANK], F32, name="angle", tag="o")
+            angle = psum_t.tile([P, BANK], F32, name="angle", tag="zT")
             for r in range(4):
                 nc.tensor.transpose(
                     angle[:, r * P : (r + 1) * P],
@@ -152,9 +159,11 @@ def tile_rotaryembeddingtransformerlayer_pa_t_kernel(
                 out=sin_tab[:, 0, h, BANK * g : BANK * (g + 1)], in_=angle[:], func=ACT.Sin, scale=parity_sign[:]
             )
 
-        def table_negate():
+        def table_negate(g):
+            cols = slice(BANK * g, BANK * (g + 1))
             nc.gpsimd.tensor_scalar(
-                out=sin_tab[:, 1], in0=sin_tab[:, 0], scalar1=-1.0, scalar2=0.0, op0=ALU.mult, op1=ALU.add
+                out=sin_tab[:, 1, :, cols], in0=sin_tab[:, 0, :, cols], scalar1=-1.0, scalar2=0.0,
+                op0=ALU.mult, op1=ALU.add,
             )
 
         def bn(t, b):
@@ -213,19 +222,21 @@ def tile_rotaryembeddingtransformerlayer_pa_t_kernel(
                 nc.scalar.activation(out=out, in_=x, func=ACT.Identity, scale=rstd, bias=shift)
 
         def transpose(t, kc):
-            zT_of[t, kc] = psum_t.tile([P, TOKENS], F32, name="zT")
+            zT_of[t, kc] = psum_t.tile([P, TOKENS], F32, name="zT", tag="zT")
             for b in range(BATCH):
                 nc.tensor.transpose(
                     zT_of[t, kc][:, b * P : (b + 1) * P], z_of[t][:, b, kc * P : (kc + 1) * P], ident[:]
                 )
 
-        def gain_out(t, kc):
+        def gain_out(t, kc, on_vector=False):
             if kc == 0:
                 planes_of[t] = plane_pool.tile([P, CHUNKS, TOKENS], BF16, name="planes")
-            nc.scalar.activation(
-                out=planes_of[t][:, kc, :], in_=zT_of[t, kc][:], func=ACT.Identity,
-                scale=gain[:, kc : kc + 1], bias=gain[:, CHUNKS + kc : CHUNKS + kc + 1],
-            )
+            out, zT = planes_of[t][:, kc, :], zT_of[t, kc][:]
+            g, be = gain[:, kc : kc + 1], gain[:, CHUNKS + kc : CHUNKS + kc + 1]
+            if on_vector:
+                nc.vector.tensor_scalar(out=out, in0=zT, scalar1=g, scalar2=be, op0=ALU.mult, op1=ALU.add)
+            else:
+                nc.scalar.activation(out=out, in_=zT, func=ACT.Identity, scale=g, bias=be)
 
         def regroup(t, c):
             if c == 0:
@@ -285,9 +296,12 @@ def tile_rotaryembeddingtransformerlayer_pa_t_kernel(
                     )
             return total
 
-        def mix_out(t, qk, b0, total):
+        def mix_out(t, qk, b0, total, on_vector=False):
             result = outs.tile([P, 2, E], F32, name="result")
-            nc.scalar.copy(out=result[:], in_=total[:])
+            if on_vector:
+                nc.vector.tensor_copy(out=result[:], in_=total[:])
+            else:
+                nc.scalar.copy(out=result[:], in_=total[:])
             out = (out_0, out_1)[qk]
             nc.sync.dma_start(out=out[b0 : b0 + 2, rows(t), :].rearrange("b p e -> p b e"), in_=result[:])
 
@@ -330,7 +344,8 @@ def tile_rotaryembeddingtransformerlayer_pa_t_kernel(
 
         def weights_turn(c, pair):
             w_words = w_rows[:].rearrange("p r k -> p (r k)").bitcast(F32).rearrange("p (r w) -> p r w", r=N_OUT // P)
-            wT = psum_acc.tile([P, 2, 2 * P], F32, name="wT", tag="acc")
+            pool, tag = (psum_acc, "acc") if c == 0 or pair == 2 else (psum_o, "o")
+            wT = pool.tile([P, 2, 2 * P], F32, name="wT", tag=tag)
             for u in range(2):
                 for h in range(2):
                     nc.tensor.transpose(
@@ -366,8 +381,8 @@ def tile_rotaryembeddingtransformerlayer_pa_t_kernel(
         nc.sync.dma_start(out=g1_bf16[:], in_=g1.rearrange("(c p j) -> p c j", c=PASSES, j=PACK))
         nc.sync.dma_start(out=be1_bf16[:], in_=be1.rearrange("(c p j) -> p c j", c=PASSES, j=PACK))
         nc.sync.dma_start(out=bias_rows[0:PACK, :], in_=bqkv[0 : 2 * E].rearrange("(r p) -> r p", p=P))
-        load(1)
         nc.sync.dma_start(out=w_rows[:], in_=Wqkv.rearrange("(r p) k -> p r k", p=P))
+        load(1)
         nc.sync.dma_start(out=bias_v[:], in_=bqkv[2 * E : N_OUT].partition_broadcast(P))
         load(2)
         table_angles()
@@ -381,79 +396,123 @@ def tile_rotaryembeddingtransformerlayer_pa_t_kernel(
             for b in (b0, b0 + 1):
                 aggregate(0, b)
             scale_and_shift(0, b0, b0 + 2)
-            normalise(0, b0, True)
-            normalise(0, b0 + 1, False)
+        for b in range(BATCH):
+            normalise(0, b, b >= S_NORM)
+        table_pairs(0)
         prepare_constants()
-        for h in range(2):
-            table_cos(h, 0)
+        for b in range(BATCH):
+            bn(1, b)
+        for b in range(BATCH):
+            aggregate(1, b)
         for kc in range(T_BANKS):
             transpose(0, kc)
-        moments(1)
+        w_tiles = [(c, pair) for c in range(PASSES) for pair in range(N_OUT // (2 * P))]
+        for c, pair in w_tiles[:5]:
+            weights_copy(c, pair, weights_turn(c, pair))
+        scale_and_shift(1, 0, BATCH)
 
-        v_accs, q_sums = [], []
-        for r in range(ROUNDS + 2):
+        q_sums, v_accs = [], []
+        for r in range(ROUNDS + 1):
             m = r - 1
             if live(r + 3):
                 load(r + 3)
-            for b0, acc in v_accs:
-                add_bias_v(m - 1, b0, acc)
-            v_accs = []
-            if live(r + 2):
-                for b in range(BATCH):
-                    bn(r + 2, b)
-                for b in range(BATCH):
-                    aggregate(r + 2, b)
-            if r == 1:
-                for pair in range(N_OUT // (2 * P)):
-                    weights_copy(1, pair, wTs[pair])
-                for c in range(PASSES):
-                    weights_quantise(c)
-                quantise(0)
+            if live(m - 1):
+                add_bias_v(m - 1, 0, v_accs[0])
             if live(r):
-                for kc in range(5):
+                for kc in range(3):
                     gain_out(r, kc)
                     transpose(r, kc + T_BANKS)
-                    if kc == 3:
-                        regroup(r, 0)
-                    if kc == 1 and r == 0:
-                        for pair in range(N_OUT // (2 * P)):
-                            weights_copy(0, pair, weights_turn(0, pair))
-            for args in q_sums:
-                mix_out(*args)
+            if live(m - 1):
+                mix_out(*q_sums[0])
+            if live(r + 2):
+                bn(r + 2, 0)
+            if live(m - 1):
+                add_bias_v(m - 1, 2, v_accs[1])
+                k_sums = [(m - 1, 1, 0, mix_back(m - 1, 1, 0))]
+            if live(r + 2):
+                bn(r + 2, 1)
+            if live(r):
+                gain_out(r, 3)
+                transpose(r, 6)
+                regroup(r, 0)
+                gain_out(r, 4)
+                transpose(r, 7)
+                if r == 0:
+                    weights_copy(*w_tiles[5], weights_turn(*w_tiles[5]))
+                    for c in range(PASSES):
+                        weights_quantise(c)
+            if live(m - 1):
+                mix_out(*q_sums[1])
+            if live(m):
+                quantise(m)
+            if live(r + 2):
+                bn(r + 2, 2)
+                bn(r + 2, 3)
+                for b in range(BATCH):
+                    aggregate(r + 2, b)
+                if r > 0:
+                    scale_and_shift(r + 2, 0, BATCH)
+                    normalise(r + 2, 3, True)
+            if live(r) and not live(r + 2):
+                for kc in range(5, CHUNKS):
+                    gain_out(r, kc, True)
             if live(m):
                 accs = [multiply_qk(m, n) for n in range(3)]
-                mix_terms(m, 0, accs[0])
-            k_sums = []
             if live(m - 1):
-                k_sums = [(m - 1, 1, b0, mix_back(m - 1, 1, b0)) for b0 in (0, 2)]
+                k_sums.append((m - 1, 1, 2, mix_back(m - 1, 1, 2)))
             if live(m):
+                mix_terms(m, 0, accs[0])
                 accs.append(multiply_qk(m, 3))
-                for n in (1, 2, 3):
+                for n in range(1, 4):
                     mix_terms(m, n, accs[n])
-            if live(r + 1):
-                for b in range(BATCH):
-                    normalise(r + 1, b, b >= S_NORM)
-            if live(r + 2):
-                scale_and_shift(r + 2, 0, BATCH)
-            if live(r):
+            if r in (0, 2):
                 for kc in range(5, CHUNKS):
                     gain_out(r, kc)
-                regroup(r, 1)
-            for args in k_sums:
-                mix_out(*args)
             if live(r + 1):
-                for kc in range(T_BANKS):
-                    transpose(r + 1, kc)
-            if live(m):
-                v_accs = [(b0, multiply_v(m, b0)) for b0 in (0, 2)]
-                q_sums = [(m, 0, b0, mix_back(m, 0, b0)) for b0 in (0, 2)]
+                for b in range(S_NORM if r > 0 else BATCH):
+                    normalise(r + 1, b, False)
+            if r in (0, 2):
+                for h in range(2):
+                    table_cos(h, r // 2)
+                for h in range(2):
+                    table_sin(h, r // 2)
+            if live(r + 2) and r not in (0, 2):
+                gain_out(r, 5)
+            if live(r + 1):
+                transpose(r + 1, 0)
+            if live(m) and live(r):
+                v_accs = [multiply_v(m, 0)]
+            for kc in (6, 7):
+                if live(r + 2) and r not in (0, 2):
+                    gain_out(r, kc)
+                if live(r + 1):
+                    transpose(r + 1, kc - 5)
+            if live(r):
+                regroup(r, 1)
+            if live(r):
+                if live(m):
+                    v_accs.append(multiply_v(m, 2))
+                    q_next = [(m, 0, b0, mix_back(m, 0, b0)) for b0 in (0, 2)]
+                if live(m - 1):
+                    for args in k_sums:
+                        mix_out(*args)
+                if live(m):
+                    q_sums = q_next
             if r == 0:
-                wTs = [weights_turn(1, pair) for pair in range(N_OUT // (2 * P))]
-                for h in range(2):
-                    table_sin(h, 0)
-                for h in range(2):
-                    table_cos(h, 1)
-                    table_sin(h, 1)
-                table_negate()
-            if live(r) and r > 0:
-                quantise(r)
+                scale_and_shift(2, 0, BATCH)
+                normalise(2, 3, True)
+                table_negate(0)
+            if r == 1:
+                table_pairs(1)
+            if r == 2:
+                table_negate(1)
+        t = ROUNDS - 1
+        for args in k_sums:
+            mix_out(*args)
+        for b0 in (0, 2):
+            mix_out(t, 0, b0, mix_back(t, 0, b0))
+        v_accs = [multiply_v(t, b0) for b0 in (0, 2)]
+        for b0 in (0, 2):
+            add_bias_v(t, b0, v_accs[b0 // 2])
+        for b0 in (0, 2):
+            mix_out(t, 1, b0, mix_back(t, 1, b0), b0 == 2)

@@ -47,7 +47,7 @@ def tile_rotaryembeddingtransformerlayer_pa_t_kernel(
     with (
         tc.tile_pool(name="const", bufs=1) as const,
         tc.tile_pool(name="work", bufs=1) as work,
-        tc.tile_pool(name="xin", bufs=3) as xin,
+        tc.tile_pool(name="xin", bufs=4) as xin,
         tc.tile_pool(name="small", bufs=3) as small,
         tc.tile_pool(name="norm", bufs=2) as norm,
         tc.tile_pool(name="planes", bufs=2) as plane_pool,
@@ -76,6 +76,8 @@ def tile_rotaryembeddingtransformerlayer_pa_t_kernel(
         g1_bf16 = work.tile([P, PASSES, PACK], BF16)
         be1_bf16 = work.tile([P, PASSES, PACK], BF16)
         bias_rows = work.tile([P, P], BF16)
+        v_row = work.tile([P, E], BF16)
+        ones = work.tile([P, P], BF16)
         bias_rows_f32 = work.tile([P, P], F32)
         turns = work.tile([P, ROUNDS, HALF], F32)
         minus_f = work.tile([P, ROUNDS, HALF], F32)
@@ -340,6 +342,11 @@ def tile_rotaryembeddingtransformerlayer_pa_t_kernel(
                 out=parity_sign[:], in0=parity_sign[:], scalar1=-2.0, scalar2=1.0, op0=ALU.mult, op1=ALU.add
             )
 
+        def spread_bias_v():
+            spread = psum_o.tile([P, E], F32, name="spread", tag="o")
+            nc.tensor.matmul(spread[:], lhsT=ones[:], rhs=v_row[:], start=True, stop=True)
+            nc.vector.tensor_copy(out=bias_v[:], in_=spread[:])
+
         w_grouped = work.tile([P, PASSES, N_OUT, PACK], BF16, name="w_grouped", align_bytes=64)
 
         def weights_turn(c, pair):
@@ -372,6 +379,8 @@ def tile_rotaryembeddingtransformerlayer_pa_t_kernel(
 
         load(0)
         nc.vector.memset(bias_rows[:], 0.0)
+        nc.vector.memset(v_row[:], 0.0)
+        nc.gpsimd.memset(ones[:], 1.0)
         nc.vector.memset(minus_half[:], -0.5)
         nc.vector.memset(quarter_turn[:], 1.0)
         nc.vector.tensor_scalar(
@@ -381,10 +390,11 @@ def tile_rotaryembeddingtransformerlayer_pa_t_kernel(
         nc.sync.dma_start(out=g1_bf16[:], in_=g1.rearrange("(c p j) -> p c j", c=PASSES, j=PACK))
         nc.sync.dma_start(out=be1_bf16[:], in_=be1.rearrange("(c p j) -> p c j", c=PASSES, j=PACK))
         nc.sync.dma_start(out=bias_rows[0:PACK, :], in_=bqkv[0 : 2 * E].rearrange("(r p) -> r p", p=P))
+        nc.sync.dma_start(out=v_row[0:1, :], in_=bqkv[2 * E : N_OUT].rearrange("(r e) -> r e", r=1))
         nc.sync.dma_start(out=w_rows[:], in_=Wqkv.rearrange("(r p) k -> p r k", p=P))
         load(1)
-        nc.sync.dma_start(out=bias_v[:], in_=bqkv[2 * E : N_OUT].partition_broadcast(P))
         load(2)
+        load(3)
         table_angles()
         make_identity(nc, ident[:])
         for g in range(2):
@@ -414,8 +424,8 @@ def tile_rotaryembeddingtransformerlayer_pa_t_kernel(
         q_sums, v_accs = [], []
         for r in range(ROUNDS + 1):
             m = r - 1
-            if live(r + 3):
-                load(r + 3)
+            if live(r + 4):
+                load(r + 4)
             if live(m - 1):
                 add_bias_v(m - 1, 0, v_accs[0])
             if live(r):
@@ -439,6 +449,7 @@ def tile_rotaryembeddingtransformerlayer_pa_t_kernel(
                 transpose(r, 7)
                 if r == 0:
                     weights_copy(*w_tiles[5], weights_turn(*w_tiles[5]))
+                    spread_bias_v()
                     for c in range(PASSES):
                         weights_quantise(c)
             if live(m - 1):

@@ -31,7 +31,7 @@ TOKENS = BATCH * P
 BN_CHUNK = 512
 BANK = 512
 T_BANKS = 3
-S_NORM = 3
+LAST = BATCH - 1
 
 FIRST_FREQS = 8
 FREQ_RATIO = 10000.0 ** (-1.0 / HALF)
@@ -184,44 +184,37 @@ def tile_rotaryembeddingtransformerlayer_pa_t_kernel(
                 out=moments_of[t][1][:, b, :], in_=moments_of[t][0][:, b, :, :].rearrange("p h s -> p (h s)")
             )
 
-        def moments(t):
-            for b in range(BATCH):
-                bn(t, b)
-            for b in range(BATCH):
-                aggregate(t, b)
-            scale_and_shift(t, 0, BATCH)
-
         def scale_and_shift(t, lo, hi):
-            n = hi - lo
             mean_var = moments_of[t][1]
             var_eps = small.tile([P, BATCH], F32, name="var_eps")
             minus_mean = small.tile([P, BATCH], F32, name="minus_mean")
-            if lo == 0:
+            if t not in rstd_of:
                 rstd_of[t] = small.tile([P, BATCH], F32, name="rstd")
                 shift_of[t] = small.tile([P, BATCH], F32, name="shift")
             nc.gpsimd.tensor_scalar(
-                out=var_eps[:, 0:n], in0=mean_var[:, lo:hi, 1], scalar1=1.0, scalar2=EPS, op0=ALU.mult, op1=ALU.add
+                out=var_eps[:, lo:hi], in0=mean_var[:, lo:hi, 1], scalar1=1.0, scalar2=EPS, op0=ALU.mult, op1=ALU.add
             )
             nc.gpsimd.tensor_scalar(
-                out=minus_mean[:, 0:n], in0=mean_var[:, lo:hi, 0], scalar1=-1.0, scalar2=0.0, op0=ALU.mult, op1=ALU.add
+                out=minus_mean[:, lo:hi], in0=mean_var[:, lo:hi, 0], scalar1=-1.0, scalar2=0.0,
+                op0=ALU.mult, op1=ALU.add,
             )
             nc.gpsimd.tensor_tensor(
-                out=rstd_of[t][:, lo:hi], in0=var_eps[:, 0:n], in1=minus_half[:, 0:n], op=ALU.pow
+                out=rstd_of[t][:, lo:hi], in0=var_eps[:, lo:hi], in1=minus_half[:, lo:hi], op=ALU.pow
             )
             nc.gpsimd.tensor_tensor(
-                out=shift_of[t][:, lo:hi], in0=minus_mean[:, 0:n], in1=rstd_of[t][:, lo:hi], op=ALU.mult
+                out=shift_of[t][:, lo:hi], in0=minus_mean[:, lo:hi], in1=rstd_of[t][:, lo:hi], op=ALU.mult
             )
 
-        def normalise(t, b, on_gpsimd):
+        def normalise(t, b, engine):
             if t not in z_of:
                 z_of[t] = norm.tile([P, BATCH, D], F32, name="z")
             out = z_of[t][:, b, :].rearrange("p (c j m) -> p c j m", c=PASSES, j=PACK)
             x = x_of[t][:, b, :].rearrange("p (c m j) -> p c j m", c=PASSES, j=PACK)
             rstd, shift = rstd_of[t][:, b : b + 1], shift_of[t][:, b : b + 1]
-            if on_gpsimd:
-                nc.gpsimd.tensor_scalar(out=out, in0=x, scalar1=rstd, scalar2=shift, op0=ALU.mult, op1=ALU.add)
-            else:
+            if engine is nc.scalar:
                 nc.scalar.activation(out=out, in_=x, func=ACT.Identity, scale=rstd, bias=shift)
+            else:
+                engine.tensor_scalar(out=out, in0=x, scalar1=rstd, scalar2=shift, op0=ALU.mult, op1=ALU.add)
 
         def transpose(t, kc):
             zT_of[t, kc] = psum_t.tile([P, TOKENS], F32, name="zT", tag="zT")
@@ -230,24 +223,19 @@ def tile_rotaryembeddingtransformerlayer_pa_t_kernel(
                     zT_of[t, kc][:, b * P : (b + 1) * P], z_of[t][:, b, kc * P : (kc + 1) * P], ident[:]
                 )
 
-        def gain_out(t, kc, on_vector=False):
+        def gain_out(t, kc):
             if kc == 0:
                 planes_of[t] = plane_pool.tile([P, CHUNKS, TOKENS], BF16, name="planes")
             out, zT = planes_of[t][:, kc, :], zT_of[t, kc][:]
             g, be = gain[:, kc : kc + 1], gain[:, CHUNKS + kc : CHUNKS + kc + 1]
-            if on_vector:
-                nc.vector.tensor_scalar(out=out, in0=zT, scalar1=g, scalar2=be, op0=ALU.mult, op1=ALU.add)
-            else:
-                nc.scalar.activation(out=out, in_=zT, func=ACT.Identity, scale=g, bias=be)
+            nc.scalar.activation(out=out, in_=zT, func=ACT.Identity, scale=g, bias=be)
 
         def regroup(t, c):
             if c == 0:
-                grouped_of[t] = quant.tile([P, PASSES, TOKENS, PACK], BF16, name="grouped", align_bytes=64)
-            nc.gpsimd.tensor_scalar(
-                out=grouped_of[t][:, c, :, :],
-                in0=planes_of[t][:, PACK * c : PACK * (c + 1), :].rearrange("p j m -> p m j"),
-                scalar1=1.0, scalar2=0.0, op0=ALU.mult, op1=ALU.add,
-            )
+                grouped_of[t] = work.tile([P, PASSES, TOKENS, PACK], BF16, name="grouped", align_bytes=64)
+            out = grouped_of[t][:, c, :, :]
+            planes = planes_of[t][:, PACK * c : PACK * (c + 1), :].rearrange("p j m -> p m j")
+            nc.gpsimd.tensor_scalar(out=out, in0=planes, scalar1=1.0, scalar2=0.0, op0=ALU.mult, op1=ALU.add)
 
         def quantise(t):
             codes_of[t] = quant.tile([P, PASSES, TOKENS], U32, name="codes", align_bytes=64)
@@ -327,13 +315,17 @@ def tile_rotaryembeddingtransformerlayer_pa_t_kernel(
             )
             nc.sync.dma_start(out=out_2[b0 : b0 + 2, rows(t), :].rearrange("b p e -> p b e"), in_=v[:])
 
-        def prepare_constants():
+        def prepare_gains():
             nc.vector.tensor_copy(out=gain[:, 0:CHUNKS], in_=g1_bf16[:].rearrange("p c j -> p (c j)"))
             nc.vector.tensor_copy(out=gain[:, CHUNKS : 2 * CHUNKS], in_=be1_bf16[:].rearrange("p c j -> p (c j)"))
+
+        def prepare_bias():
             nc.vector.tensor_copy(out=bias_rows_f32[:], in_=bias_rows[:])
             bias_ps = psum_o.tile([P, P], F32, name="bias_ps", tag="o")
             nc.tensor.transpose(bias_ps[:], bias_rows_f32[:], ident[:])
             nc.vector.tensor_copy(out=bias_col[:], in_=bias_ps[:, 0:PACK])
+
+        def prepare_parity():
             nc.vector.tensor_copy(
                 out=evens_odds[:].rearrange("p (s g) -> p s g", s=2), in_=ident[:].rearrange("p (g s) -> p s g", s=2)
             )
@@ -397,132 +389,145 @@ def tile_rotaryembeddingtransformerlayer_pa_t_kernel(
         load(3)
         table_angles()
         make_identity(nc, ident[:])
-        for g in range(2):
-            table_fractions(g)
-            table_embedding(g)
+        table_fractions(0)
+        table_embedding(0)
         for b0 in (0, 2):
             for b in (b0, b0 + 1):
                 bn(0, b)
             for b in (b0, b0 + 1):
                 aggregate(0, b)
             scale_and_shift(0, b0, b0 + 2)
-        for b in range(BATCH):
-            normalise(0, b, b >= S_NORM)
-        table_pairs(0)
-        prepare_constants()
-        for b in range(BATCH):
-            bn(1, b)
-        for b in range(BATCH):
-            aggregate(1, b)
+            if b0 == 0:
+                for h in range(2):
+                    table_cos(h, 0)
+                table_pairs(0)
+                prepare_parity()
+        for b in range(LAST):
+            normalise(0, b, nc.scalar)
+        prepare_gains()
+        table_fractions(1)
+        w_tiles = [(c, pair) for c in range(PASSES) for pair in range(N_OUT // (2 * P))]
+        wTs = [weights_turn(*w_tiles[i]) for i in range(3)]
+        for i in range(2):
+            weights_copy(*w_tiles[i], wTs[i])
+        normalise(0, LAST, nc.vector)
+        weights_copy(*w_tiles[2], wTs[2])
+        for h in range(2):
+            table_sin(h, 0)
+        table_negate(0)
         for kc in range(T_BANKS):
             transpose(0, kc)
-        w_tiles = [(c, pair) for c in range(PASSES) for pair in range(N_OUT // (2 * P))]
-        for c, pair in w_tiles[:5]:
-            weights_copy(c, pair, weights_turn(c, pair))
-        scale_and_shift(1, 0, BATCH)
+        wTs = [weights_turn(*w_tiles[i]) for i in range(3, 5)]
+        for b in range(2):
+            bn(1, b)
+        for b in range(2):
+            aggregate(1, b)
+        scale_and_shift(1, 0, 2)
+        for i in range(3, 5):
+            weights_copy(*w_tiles[i], wTs[i - 3])
+        for b in range(2, BATCH):
+            bn(1, b)
+        for b in range(2, BATCH):
+            aggregate(1, b)
+        for kc in range(CHUNKS):
+            gain_out(0, kc)
+            if kc + T_BANKS < CHUNKS:
+                transpose(0, kc + T_BANKS)
+            if kc == PACK - 1:
+                regroup(0, 0)
+                scale_and_shift(1, 2, BATCH)
+        regroup(0, 1)
+        weights_copy(*w_tiles[5], weights_turn(*w_tiles[5]))
+        prepare_bias()
+        spread_bias_v()
+        for b in range(BATCH):
+            normalise(1, b, nc.scalar)
+        for kc in range(T_BANKS):
+            transpose(1, kc)
+        load(4)
+        for b in range(BATCH):
+            bn(2, b)
+        for kc in range(PACK + 1):
+            gain_out(1, kc)
+            if kc < 2:
+                transpose(1, kc + T_BANKS)
+        for c in range(PASSES):
+            weights_quantise(c)
+        for b in range(BATCH):
+            aggregate(2, b)
+        scale_and_shift(2, 0, BATCH)
 
-        q_sums, v_accs = [], []
-        for r in range(ROUNDS + 1):
-            m = r - 1
-            if live(r + 4):
-                load(r + 4)
-            if live(m - 1):
-                add_bias_v(m - 1, 0, v_accs[0])
-            if live(r):
-                for kc in range(3):
-                    gain_out(r, kc)
-                    transpose(r, kc + T_BANKS)
-            if live(m - 1):
-                mix_out(*q_sums[0])
-            if live(r + 2):
-                bn(r + 2, 0)
-            if live(m - 1):
-                add_bias_v(m - 1, 2, v_accs[1])
-                k_sums = [(m - 1, 1, 0, mix_back(m - 1, 1, 0))]
-            if live(r + 2):
-                bn(r + 2, 1)
-            if live(r):
-                gain_out(r, 3)
-                transpose(r, 6)
-                regroup(r, 0)
-                gain_out(r, 4)
-                transpose(r, 7)
-                if r == 0:
-                    weights_copy(*w_tiles[5], weights_turn(*w_tiles[5]))
-                    spread_bias_v()
-                    for c in range(PASSES):
-                        weights_quantise(c)
-            if live(m - 1):
-                mix_out(*q_sums[1])
-            if live(m):
-                quantise(m)
-            if live(r + 2):
-                bn(r + 2, 2)
-                bn(r + 2, 3)
-                for b in range(BATCH):
-                    aggregate(r + 2, b)
-                if r > 0:
-                    scale_and_shift(r + 2, 0, BATCH)
-                    normalise(r + 2, 3, True)
-            if live(r) and not live(r + 2):
-                for kc in range(5, CHUNKS):
-                    gain_out(r, kc, True)
-            if live(m):
-                accs = [multiply_qk(m, n) for n in range(3)]
-            if live(m - 1):
-                k_sums.append((m - 1, 1, 2, mix_back(m - 1, 1, 2)))
-            if live(m):
-                mix_terms(m, 0, accs[0])
-                accs.append(multiply_qk(m, 3))
-                for n in range(1, 4):
-                    mix_terms(m, n, accs[n])
-            if r in (0, 2):
-                for kc in range(5, CHUNKS):
-                    gain_out(r, kc)
-            if live(r + 1):
-                for b in range(S_NORM if r > 0 else BATCH):
-                    normalise(r + 1, b, False)
-            if r in (0, 2):
-                for h in range(2):
-                    table_cos(h, r // 2)
-                for h in range(2):
-                    table_sin(h, r // 2)
-            if live(r + 2) and r not in (0, 2):
-                gain_out(r, 5)
-            if live(r + 1):
-                transpose(r + 1, 0)
-            if live(m) and live(r):
-                v_accs = [multiply_v(m, 0)]
-            for kc in (6, 7):
-                if live(r + 2) and r not in (0, 2):
-                    gain_out(r, kc)
-                if live(r + 1):
-                    transpose(r + 1, kc - 5)
-            if live(r):
-                regroup(r, 1)
-            if live(r):
-                if live(m):
-                    v_accs.append(multiply_v(m, 2))
-                    q_next = [(m, 0, b0, mix_back(m, 0, b0)) for b0 in (0, 2)]
-                if live(m - 1):
-                    for args in k_sums:
-                        mix_out(*args)
-                if live(m):
-                    q_sums = q_next
-            if r == 0:
-                scale_and_shift(2, 0, BATCH)
-                normalise(2, 3, True)
-                table_negate(0)
-            if r == 1:
+        for m in range(ROUNDS):
+            measure = live(m + 3)
+            if live(m + 5):
+                load(m + 5)
+            if not measure:
+                k_first = mix_back(m - 1, 1, 0)
+            quantise(m)
+            if measure:
+                bn(m + 3, 0)
+            if live(m + 1):
+                regroup(m + 1, 0)
+            if live(m + 2):
+                normalise(m + 2, LAST, nc.gpsimd if measure else nc.vector)
+                for b in range(2):
+                    normalise(m + 2, b, nc.scalar)
+            if 0 < m <= 6:
+                v_accs = [multiply_v(m - 1, b0) for b0 in (0, 2)]
+            accs = [multiply_qk(m, 0)]
+            if not measure:
+                accs += [multiply_qk(m, n) for n in (1, 2)]
+            if m > 0:
+                for b0 in (0, 2):
+                    add_bias_v(m - 1, b0, v_accs[b0 // 2])
+            mix_terms(m, 0, accs[0])
+            for i in range(3):
+                if live(m + 1) and m < 5:
+                    transpose(m + 1, 5 + i)
+                    gain_out(m + 1, 5 + i)
+                if i < 2 and m > 0:
+                    mix_out(m - 1, 1, 2 * i, mix_back(m - 1, 1, 2 * i) if i or measure else k_first)
+            if live(m + 1):
+                regroup(m + 1, 1)
+            if live(m + 2):
+                normalise(m + 2, 2, nc.scalar)
+            accs += [multiply_qk(m, n) for n in range(len(accs), 4)]
+            if m == 1:
+                table_embedding(1)
                 table_pairs(1)
-            if r == 2:
+            if m == 2:
+                for h in range(2):
+                    table_cos(h, 1)
+            if m == 3:
+                for h in range(2):
+                    table_sin(h, 1)
                 table_negate(1)
+            if measure:
+                for b in range(1, BATCH):
+                    bn(m + 3, b)
+                for b in range(BATCH):
+                    aggregate(m + 3, b)
+                scale_and_shift(m + 3, 0, BATCH)
+            for n in (1, 2, 3):
+                mix_terms(m, n, accs[n])
+            if live(m + 2):
+                for kc in range(T_BANKS):
+                    transpose(m + 2, kc)
+                for kc in range(T_BANKS):
+                    gain_out(m + 2, kc)
+                for kc in range(T_BANKS, PACK + 1):
+                    transpose(m + 2, kc)
+                    gain_out(m + 2, kc)
+            for b0 in (0, 2):
+                mix_out(m, 0, b0, mix_back(m, 0, b0))
+            if m >= 6:
+                v_accs = [multiply_v(m, b0) for b0 in (0, 2)]
+            if live(m + 2):
+                if not m + 1 < 5:
+                    for kc in range(PACK + 1, CHUNKS):
+                        transpose(m + 2, kc)
+                        gain_out(m + 2, kc)
         t = ROUNDS - 1
-        for args in k_sums:
-            mix_out(*args)
-        for b0 in (0, 2):
-            mix_out(t, 0, b0, mix_back(t, 0, b0))
-        v_accs = [multiply_v(t, b0) for b0 in (0, 2)]
         for b0 in (0, 2):
             add_bias_v(t, b0, v_accs[b0 // 2])
         for b0 in (0, 2):

@@ -32,6 +32,7 @@ BN_CHUNK = 512
 BANK = 512
 T_BANKS = 3
 LAST = BATCH - 1
+PLAIN_CHUNKS = (2, 3, 5)
 
 FIRST_FREQS = 8
 FREQ_RATIO = 10000.0 ** (-1.0 / HALF)
@@ -219,9 +220,11 @@ def tile_rotaryembeddingtransformerlayer_pa_t_kernel(
         def transpose(t, kc):
             zT_of[t, kc] = psum_t.tile([P, TOKENS], F32, name="zT", tag="zT")
             for b in range(BATCH):
-                nc.tensor.transpose(
-                    zT_of[t, kc][:, b * P : (b + 1) * P], z_of[t][:, b, kc * P : (kc + 1) * P], ident[:]
-                )
+                out, z = zT_of[t, kc][:, b * P : (b + 1) * P], z_of[t][:, b, kc * P : (kc + 1) * P]
+                if t > 0 and kc in PLAIN_CHUNKS and b >= BATCH // 2:
+                    nc.tensor.matmul(out, lhsT=z, rhs=ident[:], start=True, stop=True)
+                else:
+                    nc.tensor.transpose(out, z, ident[:])
 
         def gain_out(t, kc):
             if kc == 0:
@@ -470,7 +473,7 @@ def tile_rotaryembeddingtransformerlayer_pa_t_kernel(
                 regroup(m + 1, 0)
             if live(m + 2):
                 normalise(m + 2, LAST, nc.gpsimd if measure else nc.vector)
-                for b in range(2):
+                for b in range(LAST):
                     normalise(m + 2, b, nc.scalar)
             if 0 < m <= 6:
                 v_accs = [multiply_v(m - 1, b0) for b0 in (0, 2)]
@@ -482,15 +485,13 @@ def tile_rotaryembeddingtransformerlayer_pa_t_kernel(
                     add_bias_v(m - 1, b0, v_accs[b0 // 2])
             mix_terms(m, 0, accs[0])
             for i in range(3):
-                if live(m + 1) and m < 5:
+                if live(m + 1) and m < 4:
                     transpose(m + 1, 5 + i)
                     gain_out(m + 1, 5 + i)
                 if i < 2 and m > 0:
                     mix_out(m - 1, 1, 2 * i, mix_back(m - 1, 1, 2 * i) if i or measure else k_first)
             if live(m + 1):
                 regroup(m + 1, 1)
-            if live(m + 2):
-                normalise(m + 2, 2, nc.scalar)
             accs += [multiply_qk(m, n) for n in range(len(accs), 4)]
             if m == 1:
                 table_embedding(1)
@@ -523,7 +524,7 @@ def tile_rotaryembeddingtransformerlayer_pa_t_kernel(
             if m >= 6:
                 v_accs = [multiply_v(m, b0) for b0 in (0, 2)]
             if live(m + 2):
-                if not m + 1 < 5:
+                if not m + 1 < 4:
                     for kc in range(PACK + 1, CHUNKS):
                         transpose(m + 2, kc)
                         gain_out(m + 2, kc)

@@ -32,7 +32,7 @@ BN_CHUNK = 512
 BANK = 512
 T_BANKS = 3
 LAST = BATCH - 1
-PLAIN_CHUNKS = (2, 3, 5)
+PLAIN_CHUNKS = (2, 3)
 
 FIRST_FREQS = 8
 FREQ_RATIO = 10000.0 ** (-1.0 / HALF)
@@ -411,27 +411,27 @@ def tile_rotaryembeddingtransformerlayer_pa_t_kernel(
         table_fractions(1)
         w_tiles = [(c, pair) for c in range(PASSES) for pair in range(N_OUT // (2 * P))]
         wTs = [weights_turn(*w_tiles[i]) for i in range(3)]
-        for i in range(2):
-            weights_copy(*w_tiles[i], wTs[i])
         normalise(0, LAST, nc.vector)
-        weights_copy(*w_tiles[2], wTs[2])
         for h in range(2):
             table_sin(h, 0)
         table_negate(0)
         for kc in range(T_BANKS):
             transpose(0, kc)
-        wTs = [weights_turn(*w_tiles[i]) for i in range(3, 5)]
-        for b in range(2):
-            bn(1, b)
-        for b in range(2):
-            aggregate(1, b)
-        scale_and_shift(1, 0, 2)
-        for i in range(3, 5):
-            weights_copy(*w_tiles[i], wTs[i - 3])
-        for b in range(2, BATCH):
-            bn(1, b)
-        for b in range(2, BATCH):
-            aggregate(1, b)
+        wTs += [weights_turn(*w_tiles[i]) for i in range(3, 5)]
+        for b0 in (0, 2):
+            for b in (b0, b0 + 1):
+                bn(1, b)
+            for b in (b0, b0 + 1):
+                aggregate(1, b)
+            if b0 == 0:
+                scale_and_shift(1, 0, 2)
+        load(4)
+        for b in range(BATCH):
+            bn(2, b)
+        for b in range(BATCH):
+            aggregate(2, b)
+        for i in range(0, 5):
+            weights_copy(*w_tiles[i], wTs[i])
         for kc in range(CHUNKS):
             gain_out(0, kc)
             if kc + T_BANKS < CHUNKS:
@@ -447,52 +447,50 @@ def tile_rotaryembeddingtransformerlayer_pa_t_kernel(
             normalise(1, b, nc.scalar)
         for kc in range(T_BANKS):
             transpose(1, kc)
-        load(4)
-        for b in range(BATCH):
-            bn(2, b)
+        scale_and_shift(2, 0, BATCH)
         for kc in range(PACK + 1):
             gain_out(1, kc)
             if kc < 2:
                 transpose(1, kc + T_BANKS)
         for c in range(PASSES):
             weights_quantise(c)
-        for b in range(BATCH):
-            aggregate(2, b)
-        scale_and_shift(2, 0, BATCH)
 
+        v_accs, k_sums = [], []
         for m in range(ROUNDS):
             measure = live(m + 3)
             if live(m + 5):
                 load(m + 5)
-            if not measure:
-                k_first = mix_back(m - 1, 1, 0)
             quantise(m)
             if measure:
                 bn(m + 3, 0)
+            if live(m + 2):
+                normalise(m + 2, 0, nc.scalar)
             if live(m + 1):
                 regroup(m + 1, 0)
-            if live(m + 2):
-                normalise(m + 2, LAST, nc.gpsimd if measure else nc.vector)
-                for b in range(LAST):
-                    normalise(m + 2, b, nc.scalar)
-            if 0 < m <= 6:
+            if m > 0:
                 v_accs = [multiply_v(m - 1, b0) for b0 in (0, 2)]
             accs = [multiply_qk(m, 0)]
-            if not measure:
-                accs += [multiply_qk(m, n) for n in (1, 2)]
+            if live(m + 2):
+                normalise(m + 2, 1, nc.scalar)
             if m > 0:
                 for b0 in (0, 2):
                     add_bias_v(m - 1, b0, v_accs[b0 // 2])
             mix_terms(m, 0, accs[0])
-            for i in range(3):
-                if live(m + 1) and m < 4:
-                    transpose(m + 1, 5 + i)
-                    gain_out(m + 1, 5 + i)
-                if i < 2 and m > 0:
-                    mix_out(m - 1, 1, 2 * i, mix_back(m - 1, 1, 2 * i) if i or measure else k_first)
+            if measure:
+                bn(m + 3, 1)
+            if live(m + 2):
+                normalise(m + 2, LAST, nc.gpsimd if measure else nc.vector)
+            if live(m + 1):
+                for kc in range(PACK + 1, CHUNKS):
+                    transpose(m + 1, kc)
+                    gain_out(m + 1, kc)
+            if m > 0:
+                k_sums = [mix_back(m - 1, 1, 0)]
+            accs += [multiply_qk(m, n) for n in (1, 2)]
             if live(m + 1):
                 regroup(m + 1, 1)
-            accs += [multiply_qk(m, n) for n in range(len(accs), 4)]
+            if live(m + 2):
+                normalise(m + 2, 2, nc.scalar)
             if m == 1:
                 table_embedding(1)
                 table_pairs(1)
@@ -503,32 +501,42 @@ def tile_rotaryembeddingtransformerlayer_pa_t_kernel(
                 for h in range(2):
                     table_sin(h, 1)
                 table_negate(1)
+            if m > 0:
+                k_sums.append(mix_back(m - 1, 1, 2))
+            accs.append(multiply_qk(m, 3))
             if measure:
-                for b in range(1, BATCH):
-                    bn(m + 3, b)
+                bn(m + 3, 2)
+            mix_terms(m, 1, accs[1])
+            if measure:
+                bn(m + 3, 3)
                 for b in range(BATCH):
                     aggregate(m + 3, b)
                 scale_and_shift(m + 3, 0, BATCH)
-            for n in (1, 2, 3):
+            for n in (2, 3):
                 mix_terms(m, n, accs[n])
+            if m > 0:
+                mix_out(m - 1, 1, 0, k_sums[0])
             if live(m + 2):
                 for kc in range(T_BANKS):
                     transpose(m + 2, kc)
-                for kc in range(T_BANKS):
-                    gain_out(m + 2, kc)
-                for kc in range(T_BANKS, PACK + 1):
-                    transpose(m + 2, kc)
-                    gain_out(m + 2, kc)
-            for b0 in (0, 2):
-                mix_out(m, 0, b0, mix_back(m, 0, b0))
-            if m >= 6:
-                v_accs = [multiply_v(m, b0) for b0 in (0, 2)]
+                gain_out(m + 2, 0)
+            if m > 0:
+                mix_out(m - 1, 1, 2, k_sums[1])
             if live(m + 2):
-                if not m + 1 < 4:
-                    for kc in range(PACK + 1, CHUNKS):
-                        transpose(m + 2, kc)
-                        gain_out(m + 2, kc)
+                gain_out(m + 2, 1)
+            q_sums = [mix_back(m, 0, 0)]
+            if live(m + 2):
+                gain_out(m + 2, 2)
+                for kc in (T_BANKS, PACK):
+                    transpose(m + 2, kc)
+            q_sums.append(mix_back(m, 0, 2))
+            mix_out(m, 0, 0, q_sums[0])
+            if live(m + 2):
+                for kc in (T_BANKS, PACK):
+                    gain_out(m + 2, kc)
+            mix_out(m, 0, 2, q_sums[1])
         t = ROUNDS - 1
+        v_accs = [multiply_v(t, b0) for b0 in (0, 2)]
         for b0 in (0, 2):
             add_bias_v(t, b0, v_accs[b0 // 2])
         for b0 in (0, 2):

import math

import concourse.mybir as mybir
from concourse.masks import make_identity

F32 = mybir.dt.float32
BF16 = mybir.dt.bfloat16
I32 = mybir.dt.int32
U32 = mybir.dt.uint32
U8 = mybir.dt.uint8
FP8X4 = mybir.dt.float8_e4m3fn_x4
ALU = mybir.AluOpType
ACT = mybir.ActivationFunctionType
AX = mybir.AxisListType

P = 128
BATCH = 4
SEQ = 1024
D = 1024
E = 256
HALF = E // 2
N_OUT = 3 * E
EPS = 1e-5

PACK = 4
K_PASS = P * PACK
PASSES = D // K_PASS
CHUNKS = D // P
ROUNDS = SEQ // P
TOKENS = BATCH * P
BN_CHUNK = 512
BANK = 512
T_BANKS = 3
LAST = BATCH - 1
PLAIN_CHUNKS = (2, 3)

FIRST_FREQS = 8
FREQ_RATIO = 10000.0 ** (-1.0 / HALF)
ROUND_MAGIC = 12582912.0

FLOPS = 2 * BATCH * SEQ * D * N_OUT


def tile_rotaryembeddingtransformerlayer_pa_t_kernel(
    tc, src, Wqkv, bqkv, g1, be1, out_0, out_1, out_2
):
    nc = tc.nc
    with (
        tc.tile_pool(name="const", bufs=1) as const,
        tc.tile_pool(name="work", bufs=1) as work,
        tc.tile_pool(name="xin", bufs=4) as xin,
        tc.tile_pool(name="small", bufs=3) as small,
        tc.tile_pool(name="norm", bufs=2) as norm,
        tc.tile_pool(name="planes", bufs=2) as plane_pool,
        tc.tile_pool(name="quant", bufs=2) as quant,
        tc.tile_pool(name="mix", bufs=3) as mix,
        tc.tile_pool(name="outs", bufs=4) as outs,
        tc.psum_pool(name="psum_t", bufs=T_BANKS) as psum_t,
        tc.psum_pool(name="psum_acc", bufs=3) as psum_acc,
        tc.psum_pool(name="psum_o", bufs=2) as psum_o,
        tc.manual_schedule(),
    ):
        ident = const.tile([P, P], F32)
        evens_odds = const.tile([P, P], F32)
        minus_half = const.tile([P, BATCH], F32)
        quarter_turn = const.tile([P, 1], F32)
        parity_sign = const.tile([P, 1], F32)
        warm = const.tile([P, 1], F32)
        gain = const.tile([P, 2 * CHUNKS], F32)
        bias_col = const.tile([P, PACK], F32)
        bias_v = const.tile([P, E], BF16)
        w_codes = const.tile([P, PASSES, N_OUT], U32, align_bytes=64)
        w_scales = const.tile([P, PASSES, N_OUT], U8, align_bytes=64)
        cos_tab = const.tile([P, 2, SEQ], F32)
        sin_tab = const.tile([P, 2, 2, SEQ], F32)
        w_rows = work.tile([P, N_OUT // P, D], BF16)
        g1_bf16 = work.tile([P, PASSES, PACK], BF16)
        be1_bf16 = work.tile([P, PASSES, PACK], BF16)
        bias_rows = work.tile([P, P], BF16)
        v_row = work.tile([P, E], BF16)
        ones = work.tile([P, P], BF16)
        bias_rows_f32 = work.tile([P, P], F32)
        turns = work.tile([P, ROUNDS, HALF], F32)
        minus_f = work.tile([P, ROUNDS, HALF], F32)
        emb = work.tile([P, ROUNDS, 2, HALF], F32)
        emb_pairs = work.tile([P, ROUNDS, HALF, 2], F32)

        x_of, moments_of, rstd_of, shift_of, z_of, zT_of = {}, {}, {}, {}, {}, {}
        planes_of, grouped_of, codes_of, scales_of, terms_of = {}, {}, {}, {}, {}

        def live(t):
            return 0 <= t < ROUNDS

        def rows(t):
            return slice(t * P, (t + 1) * P)

        def load(t):
            x_of[t] = xin.tile([P, BATCH, D], BF16, name="x")
            if t == 0:
                for b in range(BATCH):
                    nc.sync.dma_start(out=x_of[t][:, b, :], in_=src[b, rows(t), :])
            else:
                nc.sync.dma_start(out=x_of[t][:], in_=src[:, rows(t), :].rearrange("b p k -> p b k"))

        def table_angles():
            position = work.tile([P, ROUNDS, 1], I32)
            nc.gpsimd.iota(position[:], pattern=[[P, ROUNDS]], base=0, channel_multiplier=1)
            for i in range(FIRST_FREQS):
                nc.vector.tensor_scalar(
                    out=turns[:, :, i : i + 1], in0=position[:], scalar1=0.5 / math.pi * FREQ_RATIO**i, scalar2=None,
                    op0=ALU.mult,
                )
            n = FIRST_FREQS
            while n < HALF:
                nc.vector.tensor_scalar(
                    out=turns[:, :, n : 2 * n], in0=turns[:, :, 0:n], scalar1=FREQ_RATIO**n, scalar2=None, op0=ALU.mult
                )
                n *= 2

        def table_fractions(g):
            half = slice(4 * g, 4 * (g + 1))
            nc.vector.tensor_scalar(
                out=minus_f[:, half], in0=turns[:, half], scalar1=ROUND_MAGIC, scalar2=None, op0=ALU.add
            )
            nc.vector.scalar_tensor_tensor(
                out=minus_f[:, half], in0=minus_f[:, half], scalar=ROUND_MAGIC, in1=turns[:, half],
                op0=ALU.subtract, op1=ALU.subtract,
            )

        def table_embedding(g):
            half = slice(4 * g, 4 * (g + 1))
            nc.scalar.activation(out=emb[:, half, 0, :], in_=minus_f[:, half], func=ACT.Sin, scale=-2.0 * math.pi)
            nc.scalar.activation(out=minus_f[:, half], in_=minus_f[:, half], func=ACT.Abs)
            nc.scalar.activation(
                out=emb[:, half, 1, :], in_=minus_f[:, half], func=ACT.Sin, scale=-2.0 * math.pi, bias=quarter_turn[:]
            )

        def table_pairs(g):
            half = slice(4 * g, 4 * (g + 1))
            nc.gpsimd.tensor_scalar(
                out=emb_pairs[:, half], in0=emb[:, half].rearrange("p t s i -> p t i s"), scalar1=1.0, scalar2=0.0,
                op0=ALU.mult, op1=ALU.add,
            )

        def table_cos(h, g):
            angle = psum_t.tile([P, BANK], F32, name="angle", tag="zT")
            for r in range(4):
                nc.tensor.transpose(angle[:, r * P : (r + 1) * P], emb[:, 4 * g + r, h, :], ident[:])
            nc.scalar.activation(
                out=cos_tab[:, h, BANK * g : BANK * (g + 1)], in_=angle[:], func=ACT.Sin, bias=quarter_turn[:]
            )

        def table_sin(h, g):
            angle = psum_t.tile([P, BANK], F32, name="angle", tag="zT")
            for r in range(4):
                nc.tensor.transpose(
                    angle[:, r * P : (r + 1) * P],
                    emb_pairs[:, 4 * g + r, 64 * h : 64 * (h + 1), :].rearrange("p i s -> p (i s)"),
                    ident[:],
                )
            nc.scalar.activation(
                out=sin_tab[:, 0, h, BANK * g : BANK * (g + 1)], in_=angle[:], func=ACT.Sin, scale=parity_sign[:]
            )

        def table_negate(g):
            cols = slice(BANK * g, BANK * (g + 1))
            nc.gpsimd.tensor_scalar(
                out=sin_tab[:, 1, :, cols], in0=sin_tab[:, 0, :, cols], scalar1=-1.0, scalar2=0.0,
                op0=ALU.mult, op1=ALU.add,
            )

        def bn(t, b):
            if b == 0:
                moments_of[t] = (
                    small.tile([P, BATCH, D // BN_CHUNK, 6], F32, name="stats"),
                    small.tile([P, BATCH, 2], F32, name="mean_var"),
                )
            for h in range(D // BN_CHUNK):
                nc.vector.bn_stats(
                    out=moments_of[t][0][:, b, h, :], in_=x_of[t][:, b, h * BN_CHUNK : (h + 1) * BN_CHUNK]
                )

        def aggregate(t, b):
            nc.vector.bn_aggr(
                out=moments_of[t][1][:, b, :], in_=moments_of[t][0][:, b, :, :].rearrange("p h s -> p (h s)")
            )

        def scale_and_shift(t, lo, hi):
            mean_var = moments_of[t][1]
            var_eps = small.tile([P, BATCH], F32, name="var_eps")
            minus_mean = small.tile([P, BATCH], F32, name="minus_mean")
            if t not in rstd_of:
                rstd_of[t] = small.tile([P, BATCH], F32, name="rstd")
                shift_of[t] = small.tile([P, BATCH], F32, name="shift")
            nc.gpsimd.tensor_scalar(
                out=var_eps[:, lo:hi], in0=mean_var[:, lo:hi, 1], scalar1=1.0, scalar2=EPS, op0=ALU.mult, op1=ALU.add
            )
            nc.gpsimd.tensor_scalar(
                out=minus_mean[:, lo:hi], in0=mean_var[:, lo:hi, 0], scalar1=-1.0, scalar2=0.0,
                op0=ALU.mult, op1=ALU.add,
            )
            nc.gpsimd.tensor_tensor(
                out=rstd_of[t][:, lo:hi], in0=var_eps[:, lo:hi], in1=minus_half[:, lo:hi], op=ALU.pow
            )
            nc.gpsimd.tensor_tensor(
                out=shift_of[t][:, lo:hi], in0=minus_mean[:, lo:hi], in1=rstd_of[t][:, lo:hi], op=ALU.mult
            )

        def normalise(t, b, engine):
            if t not in z_of:
                z_of[t] = norm.tile([P, BATCH, D], F32, name="z")
            out = z_of[t][:, b, :].rearrange("p (c j m) -> p c j m", c=PASSES, j=PACK)
            x = x_of[t][:, b, :].rearrange("p (c m j) -> p c j m", c=PASSES, j=PACK)
            rstd, shift = rstd_of[t][:, b : b + 1], shift_of[t][:, b : b + 1]
            if engine is nc.scalar:
                nc.scalar.activation(out=out, in_=x, func=ACT.Identity, scale=rstd, bias=shift)
            else:
                engine.tensor_scalar(out=out, in0=x, scalar1=rstd, scalar2=shift, op0=ALU.mult, op1=ALU.add)

        def transpose(t, kc):
            zT_of[t, kc] = psum_t.tile([P, TOKENS], F32, name="zT", tag="zT")
            for b in range(BATCH):
                out, z = zT_of[t, kc][:, b * P : (b + 1) * P], z_of[t][:, b, kc * P : (kc + 1) * P]
                if t > 0 and kc in PLAIN_CHUNKS and b >= BATCH // 2:
                    nc.tensor.matmul(out, lhsT=z, rhs=ident[:], start=True, stop=True)
                else:
                    nc.tensor.transpose(out, z, ident[:])

        def gain_out(t, kc):
            if kc == 0:
                planes_of[t] = plane_pool.tile([P, CHUNKS, TOKENS], BF16, name="planes")
            out, zT = planes_of[t][:, kc, :], zT_of[t, kc][:]
            g, be = gain[:, kc : kc + 1], gain[:, CHUNKS + kc : CHUNKS + kc + 1]
            nc.scalar.activation(out=out, in_=zT, func=ACT.Identity, scale=g, bias=be)

        def regroup(t, c):
            if c == 0:
                grouped_of[t] = work.tile([P, PASSES, TOKENS, PACK], BF16, name="grouped", align_bytes=64)
            out = grouped_of[t][:, c, :, :]
            planes = planes_of[t][:, PACK * c : PACK * (c + 1), :].rearrange("p j m -> p m j")
            nc.gpsimd.tensor_scalar(out=out, in0=planes, scalar1=1.0, scalar2=0.0, op0=ALU.mult, op1=ALU.add)

        def quantise(t):
            codes_of[t] = quant.tile([P, PASSES, TOKENS], U32, name="codes", align_bytes=64)
            scales_of[t] = quant.tile([P, PASSES, TOKENS], U8, name="scales", align_bytes=64)
            nc.vector.quantize_mx(
                out=codes_of[t][:].rearrange("p c w -> p (c w)").bitcast(FP8X4),
                scales=scales_of[t][:].rearrange("p c w -> p (c w)"),
                in_=grouped_of[t][:].rearrange("p c w j -> p (c w j)"),
            )

        def multiply_qk(t, n):
            acc = psum_acc.tile([P, BANK], F32, name="acc", tag="acc")
            cols = slice(n * P, (n + 1) * P)
            for c in range(PASSES):
                nc.tensor.matmul_mx(
                    out=acc[:],
                    lhsT=w_codes[:, c, cols].bitcast(FP8X4), lhsT_scale=w_scales[:, c, cols],
                    rhs=codes_of[t][:, c, :].bitcast(FP8X4), rhs_scale=scales_of[t][:, c, :],
                    start=(c == 0), stop=(c == PASSES - 1),
                )
            return acc

        def mix_terms(t, n, acc):
            qk, h = divmod(n, 2)
            if h == 0:
                terms_of[t, qk] = mix.tile([P, 2, 2, BATCH, P], F32, name="terms")
            for term, table in ((0, cos_tab[:, h, rows(t)]), (1, sin_tab[:, qk, h, rows(t)])):
                nc.vector.scalar_tensor_tensor(
                    out=terms_of[t, qk][:, term, h], in0=acc[:].rearrange("p (b s) -> p b s", b=BATCH),
                    scalar=bias_col[:, n : n + 1], in1=table.unsqueeze(1).to_broadcast([P, BATCH, P]),
                    op0=ALU.add, op1=ALU.mult,
                )

        def mix_back(t, qk, b0):
            terms = terms_of[t, qk]
            total = psum_o.tile([P, 2, E], F32, name="total", tag="o")
            for b in range(2):
                for h in range(2):
                    nc.tensor.matmul(
                        out=total[:, b, h * P : (h + 1) * P], lhsT=terms[:, 0, h, b0 + b, :], rhs=ident[:],
                        start=(h == 0), stop=False, is_transpose=True,
                    )
                for h in range(2):
                    nc.tensor.matmul(
                        out=total[:, b, :].rearrange("p (s m g) -> p m s g", s=2, m=2)[:, h],
                        lhsT=terms[:, 1, h, b0 + b, :], rhs=evens_odds[:],
                        start=False, stop=(h == 1), is_transpose=True,
                    )
            return total

        def mix_out(t, qk, b0, total, on_vector=False):
            result = outs.tile([P, 2, E], F32, name="result")
            if on_vector:
                nc.vector.tensor_copy(out=result[:], in_=total[:])
            else:
                nc.scalar.copy(out=result[:], in_=total[:])
            out = (out_0, out_1)[qk]
            nc.sync.dma_start(out=out[b0 : b0 + 2, rows(t), :].rearrange("b p e -> p b e"), in_=result[:])

        def multiply_v(t, b0):
            acc = psum_acc.tile([P, 2, E], F32, name="acc_v", tag="acc")
            for b in range(2):
                tok = slice((b0 + b) * P, (b0 + b + 1) * P)
                for c in range(PASSES):
                    nc.tensor.matmul_mx(
                        out=acc[:, b, :],
                        lhsT=codes_of[t][:, c, tok].bitcast(FP8X4), lhsT_scale=scales_of[t][:, c, tok],
                        rhs=w_codes[:, c, 2 * E : N_OUT].bitcast(FP8X4), rhs_scale=w_scales[:, c, 2 * E : N_OUT],
                        start=(c == 0), stop=(c == PASSES - 1),
                    )
            return acc

        def add_bias_v(t, b0, acc):
            v = outs.tile([P, 2, E], F32, name="v")
            nc.vector.tensor_tensor(
                out=v[:], in0=acc[:], in1=bias_v[:].unsqueeze(1).to_broadcast([P, 2, E]), op=ALU.add
            )
            nc.sync.dma_start(out=out_2[b0 : b0 + 2, rows(t), :].rearrange("b p e -> p b e"), in_=v[:])

        def prepare_gains():
            nc.vector.tensor_copy(out=gain[:, 0:CHUNKS], in_=g1_bf16[:].rearrange("p c j -> p (c j)"))
            nc.vector.tensor_copy(out=gain[:, CHUNKS : 2 * CHUNKS], in_=be1_bf16[:].rearrange("p c j -> p (c j)"))

        def prepare_bias():
            nc.vector.tensor_copy(out=bias_rows_f32[:], in_=bias_rows[:])
            bias_ps = psum_o.tile([P, P], F32, name="bias_ps", tag="o")
            nc.tensor.transpose(bias_ps[:], bias_rows_f32[:], ident[:])
            nc.vector.tensor_copy(out=bias_col[:], in_=bias_ps[:, 0:PACK])

        def prepare_parity():
            nc.vector.tensor_copy(
                out=evens_odds[:].rearrange("p (s g) -> p s g", s=2), in_=ident[:].rearrange("p (g s) -> p s g", s=2)
            )
            nc.vector.reduce_sum(out=parity_sign[:], in_=ident[:, 0:P:2], axis=AX.X)
            nc.vector.tensor_scalar(
                out=parity_sign[:], in0=parity_sign[:], scalar1=-2.0, scalar2=1.0, op0=ALU.mult, op1=ALU.add
            )

        def spread_bias_v():
            spread = psum_o.tile([P, E], F32, name="spread", tag="o")
            nc.tensor.matmul(spread[:], lhsT=ones[:], rhs=v_row[:], start=True, stop=True)
            nc.vector.tensor_copy(out=bias_v[:], in_=spread[:])

        w_grouped = work.tile([P, PASSES, N_OUT, PACK], BF16, name="w_grouped", align_bytes=64)

        def weights_turn(c, pair):
            w_words = w_rows[:].rearrange("p r k -> p (r k)").bitcast(F32).rearrange("p (r w) -> p r w", r=N_OUT // P)
            pool, tag = (psum_acc, "acc") if c == 0 or pair == 2 else (psum_o, "o")
            wT = pool.tile([P, 2, 2 * P], F32, name="wT", tag=tag)
            for u in range(2):
                for h in range(2):
                    nc.tensor.transpose(
                        wT[:, u, h * P : (h + 1) * P],
                        w_words[:, 2 * pair + h, 2 * P * c + u : 2 * P * (c + 1) : 2],
                        ident[:],
                    )
            return wT

        def weights_copy(c, pair, wT):
            nc.vector.tensor_copy(
                out=w_grouped[:, c, 2 * P * pair : 2 * P * (pair + 1), :]
                .rearrange("p n j -> p (n j)").bitcast(F32).rearrange("p (n u) -> p n u", u=2),
                in_=wT[:].rearrange("p u n -> p n u"),
            )

        def weights_quantise(c):
            for lo, hi in ((0, 2 * E), (2 * E, N_OUT)):
                nc.vector.quantize_mx(
                    out=w_codes[:, c, lo:hi].bitcast(FP8X4),
                    scales=w_scales[:, c, lo:hi],
                    in_=w_grouped[:, c, lo:hi, :].rearrange("p n j -> p (n j)"),
                )

        load(0)
        nc.vector.memset(bias_rows[:], 0.0)
        nc.vector.memset(v_row[:], 0.0)
        nc.gpsimd.memset(ones[:], 1.0)
        nc.vector.memset(minus_half[:], -0.5)
        nc.vector.memset(quarter_turn[:], 1.0)
        nc.vector.tensor_scalar(
            out=quarter_turn[:], in0=quarter_turn[:], scalar1=0.5 * math.pi, scalar2=None, op0=ALU.mult
        )
        nc.scalar.activation(out=warm[:], in_=quarter_turn[:], func=ACT.Sin)
        nc.sync.dma_start(out=g1_bf16[:], in_=g1.rearrange("(c p j) -> p c j", c=PASSES, j=PACK))
        nc.sync.dma_start(out=be1_bf16[:], in_=be1.rearrange("(c p j) -> p c j", c=PASSES, j=PACK))
        nc.sync.dma_start(out=bias_rows[0:PACK, :], in_=bqkv[0 : 2 * E].rearrange("(r p) -> r p", p=P))
        nc.sync.dma_start(out=v_row[0:1, :], in_=bqkv[2 * E : N_OUT].rearrange("(r e) -> r e", r=1))
        nc.sync.dma_start(out=w_rows[:], in_=Wqkv.rearrange("(r p) k -> p r k", p=P))
        load(1)
        load(2)
        load(3)
        table_angles()
        make_identity(nc, ident[:])
        table_fractions(0)
        table_embedding(0)
        for b0 in (0, 2):
            for b in (b0, b0 + 1):
                bn(0, b)
            for b in (b0, b0 + 1):
                aggregate(0, b)
            scale_and_shift(0, b0, b0 + 2)
            if b0 == 0:
                for h in range(2):
                    table_cos(h, 0)
                table_pairs(0)
                prepare_parity()
        for b in range(LAST):
            normalise(0, b, nc.scalar)
        prepare_gains()
        table_fractions(1)
        w_tiles = [(c, pair) for c in range(PASSES) for pair in range(N_OUT // (2 * P))]
        wTs = [weights_turn(*w_tiles[i]) for i in range(3)]
        normalise(0, LAST, nc.vector)
        for h in range(2):
            table_sin(h, 0)
        table_negate(0)
        for kc in range(T_BANKS):
            transpose(0, kc)
        wTs += [weights_turn(*w_tiles[i]) for i in range(3, 5)]
        for b0 in (0, 2):
            for b in (b0, b0 + 1):
                bn(1, b)
            for b in (b0, b0 + 1):
                aggregate(1, b)
            if b0 == 0:
                scale_and_shift(1, 0, 2)
        load(4)
        for b in range(BATCH):
            bn(2, b)
        for b in range(BATCH):
            aggregate(2, b)
        for i in range(0, 5):
            weights_copy(*w_tiles[i], wTs[i])
        for kc in range(CHUNKS):
            gain_out(0, kc)
            if kc + T_BANKS < CHUNKS:
                transpose(0, kc + T_BANKS)
            if kc == PACK - 1:
                regroup(0, 0)
                scale_and_shift(1, 2, BATCH)
        regroup(0, 1)
        weights_copy(*w_tiles[5], weights_turn(*w_tiles[5]))
        prepare_bias()
        spread_bias_v()
        for b in range(BATCH):
            normalise(1, b, nc.scalar)
        for kc in range(T_BANKS):
            transpose(1, kc)
        scale_and_shift(2, 0, BATCH)
        for kc in range(PACK + 1):
            gain_out(1, kc)
            if kc < 2:
                transpose(1, kc + T_BANKS)
        for c in range(PASSES):
            weights_quantise(c)

        v_accs, k_sums = [], []
        for m in range(ROUNDS):
            measure = live(m + 3)
            if live(m + 5):
                load(m + 5)
            quantise(m)
            if measure:
                bn(m + 3, 0)
            if live(m + 2):
                normalise(m + 2, 0, nc.scalar)
            if live(m + 1):
                regroup(m + 1, 0)
            if m > 0:
                v_accs = [multiply_v(m - 1, b0) for b0 in (0, 2)]
            accs = [multiply_qk(m, 0)]
            if live(m + 2):
                normalise(m + 2, 1, nc.scalar)
            if m > 0:
                for b0 in (0, 2):
                    add_bias_v(m - 1, b0, v_accs[b0 // 2])
            mix_terms(m, 0, accs[0])
            if measure:
                bn(m + 3, 1)
            if live(m + 2):
                normalise(m + 2, LAST, nc.gpsimd if measure else nc.vector)
            if live(m + 1):
                for kc in range(PACK + 1, CHUNKS):
                    transpose(m + 1, kc)
                    gain_out(m + 1, kc)
            if m > 0:
                k_sums = [mix_back(m - 1, 1, 0)]
            accs += [multiply_qk(m, n) for n in (1, 2)]
            if live(m + 1):
                regroup(m + 1, 1)
            if live(m + 2):
                normalise(m + 2, 2, nc.scalar)
            if m == 1:
                table_embedding(1)
                table_pairs(1)
            if m == 2:
                for h in range(2):
                    table_cos(h, 1)
            if m == 3:
                for h in range(2):
                    table_sin(h, 1)
                table_negate(1)
            if m > 0:
                k_sums.append(mix_back(m - 1, 1, 2))
            accs.append(multiply_qk(m, 3))
            if measure:
                bn(m + 3, 2)
            mix_terms(m, 1, accs[1])
            if measure:
                bn(m + 3, 3)
                for b in range(BATCH):
                    aggregate(m + 3, b)
                scale_and_shift(m + 3, 0, BATCH)
            for n in (2, 3):
                mix_terms(m, n, accs[n])
            if m > 0:
                mix_out(m - 1, 1, 0, k_sums[0])
            if live(m + 2):
                for kc in range(T_BANKS):
                    transpose(m + 2, kc)
                gain_out(m + 2, 0)
            if m > 0:
                mix_out(m - 1, 1, 2, k_sums[1])
            if live(m + 2):
                gain_out(m + 2, 1)
            q_sums = [mix_back(m, 0, 0)]
            if live(m + 2):
                gain_out(m + 2, 2)
                for kc in (T_BANKS, PACK):
                    transpose(m + 2, kc)
            q_sums.append(mix_back(m, 0, 2))
            mix_out(m, 0, 0, q_sums[0])
            if live(m + 2):
                for kc in (T_BANKS, PACK):
                    gain_out(m + 2, kc)
            mix_out(m, 0, 2, q_sums[1])
        t = ROUNDS - 1
        v_accs = [multiply_v(t, b0) for b0 in (0, 2)]
        for b0 in (0, 2):
            add_bias_v(t, b0, v_accs[b0 // 2])
        for b0 in (0, 2):
            mix_out(t, 1, b0, mix_back(t, 1, b0), b0 == 2)
